import numpy as np
import ml_dtypes


def mxq(x, axis, fmt="e4m3"):
    dtype, down = {"e4m3": (ml_dtypes.float8_e4m3fn, 7), "e5m2": (ml_dtypes.float8_e5m2, 14)}[fmt]
    v = np.moveaxis(np.asarray(x, np.float32).astype(ml_dtypes.bfloat16).astype(np.float64), axis, -1)
    blocks = v.reshape(v.shape[:-1] + (-1, 32))
    amax = np.abs(blocks).max(-1, keepdims=True)
    byte = np.maximum(np.where(amax > 0, np.frexp(amax)[1] - 1 + 127, 0) - down, 1)
    scale = np.exp2(byte - 127.0)
    codes = (blocks / scale).astype(np.float32).astype(dtype).astype(np.float64)
    return np.moveaxis((codes * scale).reshape(v.shape), -1, axis)


WIDE = False


def mx_kscale(k):
    if not WIDE:
        return np.ones(k)
    levels = np.array([10, -10, 5, -5, 0])
    a = np.random.permutation(np.resize(levels, k // 512 * 4)).reshape(k // 512, 4)
    idx = np.arange(k)
    return np.exp2(a[idx // 512, idx % 128 // 32])


BF16 = ml_dtypes.bfloat16


def bf(x):
    return np.asarray(x, np.float32).astype(BF16)


def f64(x):
    return np.asarray(x).astype(np.float64)


N, D, M, P = 16384, 8, 512, 256


def setup_inputs():
    a = np.log2(mx_kscale(M))
    a = a.max() - a
    x = np.random.standard_normal((N, D))
    z = np.random.uniform(0.0, 1.0, (M, D))
    z[:, 0] += a * np.log(2.0)
    g = np.random.standard_normal((M, P)) * 3.2 / np.sqrt(M)
    c = np.triu(g) + 0.25 * np.tril(g, -1) + np.eye(M, P)
    return {"x": bf(x), "design_points": bf(z), "chol_inv": bf(c * np.exp2(a)[:, None])}


def reference(x, design_points, chol_inv):
    x = f64(x)
    z = f64(design_points)
    mn = np.min(x, axis=0, keepdims=True)
    mx = np.max(x, axis=0, keepdims=True)
    xs = (x - mn) / (mx - mn)
    l1 = np.zeros((x.shape[0], z.shape[0]))
    for d in range(D):
        l1 = l1 + np.abs(xs[:, d][:, None] - z[:, d][None, :])
    k_star = np.exp(-l1)
    return mxq(k_star, 1, "e4m3") @ mxq(f64(chol_inv), 0, "e4m3")

@@ -1,0 +1,271 @@
+from contextlib import ExitStack
+
+import concourse.bass as bass
+import concourse.mybir as mybir
+import concourse.tile as tile
+from concourse.masks import make_identity
+
+F32 = mybir.dt.float32
+BF16 = mybir.dt.bfloat16
+U32 = mybir.dt.uint32
+U8 = mybir.dt.uint8
+FP8X4 = mybir.dt.float8_e4m3fn_x4
+ALU = mybir.AluOpType
+ACTF = mybir.ActivationFunctionType
+AX = mybir.AxisListType
+
+P = 128
+N, D, M, PO = 16384, 8, 512, 256
+NT = N // P
+PACK = 4
+GROUP = 4
+NG = NT // GROUP
+FLOPS = 2 * N * M * PO
+
+DVE_DIMS = (0, 1, 2)
+POOL_DIMS = (3, 4, 5)
+ACT_DIMS = (6, 7)
+NMAX = 6
+BIG = 3.0e38
+
+
+def tile_tmgp_sg_t_kernel(tc, x, design_points, chol_inv, out):
+    nc = tc.nc
+    with ExitStack() as ctx:
+        consts = ctx.enter_context(tc.tile_pool(name="consts", bufs=1))
+        zbank = ctx.enter_context(tc.psum_pool(name="zbank", bufs=1))
+        ltp = ctx.enter_context(tc.psum_pool(name="ltp", bufs=3))
+        pop = ctx.enter_context(tc.psum_pool(name="pop", bufs=2))
+        accp = ctx.enter_context(tc.tile_pool(name="accp", bufs=6))
+        tactp = ctx.enter_context(tc.tile_pool(name="tactp", bufs=12))
+        tpoolp = ctx.enter_context(tc.tile_pool(name="tpoolp", bufs=18))
+        kgp = ctx.enter_context(tc.tile_pool(name="kgp", bufs=3))
+        qp = ctx.enter_context(tc.tile_pool(name="qp", bufs=3))
+        obp = ctx.enter_context(tc.tile_pool(name="obp", bufs=3))
+
+        z_sb = consts.tile([P, PACK, D], BF16)
+        nc.sync.dma_start(out=z_sb[:], in_=design_points.rearrange("(p t) d -> p t d", t=PACK))
+        x_sb = consts.tile([P, NT, D], BF16)
+        nc.sync.dma_start(out=x_sb[:], in_=x.rearrange("(p i) d -> p i d", p=P))
+        c_sb = consts.tile([P, PACK, PO], BF16)
+        nc.sync.dma_start(out=c_sb[:], in_=chol_inv.rearrange("(p t) w -> p t w", t=PACK))
+
+        ident = consts.tile([P, P], F32)
+        make_identity(nc, ident[:])
+
+        warm = consts.tile([P, 1], F32)
+        nc.vector.memset(warm[:], 0.0)
+        nc.scalar.activation(out=warm[:], in_=warm[:], func=ACTF.Exp)
+
+        zf = consts.tile([P, PACK, D], F32)
+        nc.vector.tensor_copy(out=zf[:], in_=z_sb[:])
+        z2 = consts.tile([P, PACK, D], F32)
+        nc.vector.tensor_scalar(out=z2[:], in0=zf[:], scalar1=2.0, scalar2=None, op0=ALU.mult)
+        zsum = consts.tile([P, PACK], F32)
+        nc.vector.tensor_reduce(out=zsum[:], in_=zf[:, :, 0:NMAX], axis=AX.X, op=ALU.add)
+        rz = consts.tile([P, PACK], F32)
+        nc.vector.tensor_scalar(out=rz[:], in0=zsum[:], scalar1=-1.0, scalar2=None, op0=ALU.mult)
+
+        def spread(bank, column_of):
+            for t in range(PACK):
+                nc.tensor.transpose(
+                    out=bank[:, t * P : (t + 1) * P],
+                    in_=column_of(t).to_broadcast([P, P]),
+                    identity=ident[:],
+                )
+
+        zc = {}
+        for d in DVE_DIMS:
+            zres = zbank.tile([P, M], F32, name="zres%d" % d)
+            spread(zres, lambda t, d=d: z2[:, t, d : d + 1])
+            zc[d] = zres
+        turn = 0
+        for d in POOL_DIMS + ACT_DIMS + (D,):
+            tmp = ltp.tile([P, M], F32, tag="lt", name="ztmp%d" % d)
+            if d == D:
+                spread(tmp, lambda t: rz[:, t : t + 1])
+            elif d in POOL_DIMS:
+                spread(tmp, lambda t, d=d: z2[:, t, d : d + 1])
+            else:
+                spread(tmp, lambda t, d=d: zf[:, t, d : d + 1])
+            zs = consts.tile([P, M], F32, name="zs%d" % d)
+            if turn % 2 == 0:
+                nc.scalar.copy(out=zs[:], in_=tmp[:])
+            else:
+                nc.vector.tensor_copy(out=zs[:], in_=tmp[:])
+            turn += 1
+            zc[d] = zs
+        rc = zc[D]
+
+        cg = consts.tile([P, PO, PACK], BF16, align_bytes=64)
+        nc.vector.tensor_copy(out=cg[:], in_=c_sb[:].rearrange("p t w -> p w t"))
+        c_codes = consts.tile([P, PO], U32, align_bytes=64)
+        c_scales = consts.tile([P, PO], U8, align_bytes=64)
+        nc.vector.quantize_mx(
+            out=c_codes[:].bitcast(FP8X4),
+            scales=c_scales[:],
+            in_=cg[:].rearrange("p w t -> p (w t)"),
+        )
+
+        st = consts.tile([P, P], F32)
+        nc.vector.memset(st[:], 0.0)
+        xdi = x_sb[:].rearrange("p i d -> p d i")
+        nc.vector.tensor_reduce(out=st[:, 0:D], in_=xdi, axis=AX.X, op=ALU.max)
+        mnp = consts.tile([P, D], F32)
+        nc.vector.tensor_reduce(out=mnp[:], in_=xdi, axis=AX.X, op=ALU.min)
+        nc.vector.tensor_scalar(out=st[:, D : 2 * D], in0=mnp[:], scalar1=-1.0, scalar2=None, op0=ALU.mult)
+        stT = pop.tile([P, M], F32, tag="po", name="stT")
+        nc.tensor.transpose(out=stT[:, 0:P], in_=st[:], identity=ident[:])
+        gcol = consts.tile([P, 1], F32)
+        nc.vector.tensor_reduce(out=gcol[:], in_=stT[:, 0:P], axis=AX.X, op=ALU.max)
+        gb = pop.tile([P, M], F32, tag="po", name="gb")
+        nc.tensor.transpose(out=gb[:, 0:P], in_=gcol[:, 0:1].to_broadcast([P, P]), identity=ident[:])
+        gs = consts.tile([P, 2 * D], F32)
+        nc.vector.tensor_copy(out=gs[:], in_=gb[:, 0 : 2 * D])
+        rng = consts.tile([P, D], F32)
+        nc.vector.tensor_tensor(out=rng[:], in0=gs[:, 0:D], in1=gs[:, D : 2 * D], op=ALU.add)
+        rinv = consts.tile([P, D], F32)
+        nc.vector.reciprocal(out=rinv[:], in_=rng[:])
+        r2 = consts.tile([P, D], F32)
+        nc.vector.tensor_scalar(out=r2[:], in0=rinv[:], scalar1=2.0, scalar2=None, op0=ALU.mult)
+        rneg = consts.tile([P, D], F32)
+        nc.vector.tensor_scalar(out=rneg[:], in0=rinv[:], scalar1=-1.0, scalar2=None, op0=ALU.mult)
+
+        def over_tiles(v):
+            return v.unsqueeze(1).to_broadcast([P, NT, D])
+
+        xm = consts.tile([P, NT, D], F32)
+        nc.vector.tensor_tensor(out=xm[:], in0=x_sb[:], in1=over_tiles(gs[:, D : 2 * D]), op=ALU.add)
+        x2 = consts.tile([P, NT, D], F32)
+        nc.vector.tensor_tensor(out=x2[:], in0=xm[:], in1=over_tiles(r2[:]), op=ALU.mult)
+        nx = consts.tile([P, NT, D], F32)
+        nc.vector.tensor_tensor(out=nx[:], in0=xm[:], in1=over_tiles(rneg[:]), op=ALU.mult)
+        rho = consts.tile([P, NT], F32)
+        nc.vector.tensor_reduce(out=rho[:], in_=nx[:, :, 0:NMAX], axis=AX.X, op=ALU.add)
+
+        out_v = out.rearrange("(p i) w -> p i w", p=P)
+
+        acc = {}
+        tact = {}
+        tpool = {}
+        lts = {}
+        kgs = {}
+        qs = {}
+        pos = {}
+
+        def dve_start(i):
+            a = accp.tile([P, M], F32, tag="acc", name="acc%d" % i)
+            nc.vector.tensor_scalar(out=a[:], in0=rc[:], scalar1=rho[:, i : i + 1], scalar2=None, op0=ALU.add)
+            acc[i] = a
+
+        def dve_step(i, d):
+            a = acc[i]
+            nc.vector.scalar_tensor_tensor(
+                out=a[:], in0=zc[d][:], scalar=x2[:, i, d : d + 1], in1=a[:], op0=ALU.max, op1=ALU.add
+            )
+
+        def act_terms(i):
+            tact[i] = []
+            for d in ACT_DIMS:
+                tt = tactp.tile([P, M], F32, tag="tact", name="tact%d_%d" % (i, d))
+                nc.scalar.activation(out=tt[:], in_=zc[d][:], func=ACTF.Abs, bias=nx[:, i, d : d + 1], scale=1.0)
+                tact[i].append(tt)
+
+        def pool_terms(i):
+            tpool[i] = []
+            for d in POOL_DIMS:
+                tt = tpoolp.tile([P, M], F32, tag="tpool", name="tpool%d_%d" % (i, d))
+                nc.gpsimd.tensor_scalar(
+                    out=tt[:], in0=zc[d][:], scalar1=BIG, scalar2=x2[:, i, d : d + 1], op0=ALU.min, op1=ALU.max
+                )
+                tpool[i].append(tt)
+
+        def transposes(i):
+            lt = ltp.tile([P, M], F32, tag="lt", name="lt%d" % i)
+            srcs = tpool[i] + tact[i] + [acc[i]]
+            for t in range(PACK):
+                cols = slice(t * P, (t + 1) * P)
+                for j, s in enumerate(srcs):
+                    nc.tensor.matmul(
+                        out=lt[:, cols],
+                        lhsT=s[:, cols],
+                        rhs=ident[:],
+                        start=(j == 0),
+                        stop=(j == len(srcs) - 1),
+                        is_transpose=True,
+                    )
+            lts[i] = lt
+
+        def expo(i):
+            g, s = divmod(i, GROUP)
+            if s == 0:
+                kgs[g] = kgp.tile([P, GROUP, P, PACK], BF16, tag="kg", name="kg%d" % g, align_bytes=64)
+            lt = lts[i]
+            nc.scalar.activation(
+                out=kgs[g][:, s, :, :],
+                in_=lt[:].rearrange("p (t n) -> p n t", t=PACK),
+                func=ACTF.Exp,
+                scale=-1.0,
+            )
+
+        def quantise(g):
+            codes = qp.tile([P, GROUP * P], U32, tag="codes", name="codes%d" % g, align_bytes=64)
+            scales = qp.tile([P, GROUP * P], U8, tag="scales", name="scales%d" % g, align_bytes=64)
+            nc.vector.quantize_mx(
+                out=codes[:].bitcast(FP8X4),
+                scales=scales[:],
+                in_=kgs[g][:].rearrange("p s n t -> p (s n t)"),
+            )
+            qs[g] = (codes, scales)
+
+        def multiply(g):
+            codes, scales = qs[g]
+            pos[g] = []
+            for h in range(GROUP // 2):
+                po = pop.tile([P, 2, PO], F32, tag="po", name="po%d_%d" % (g, h))
+                for e in range(2):
+                    cols = slice((2 * h + e) * P, (2 * h + e + 1) * P)
+                    nc.tensor.matmul_mx(
+                        out=po[:, e, :],
+                        lhsT=codes[:, cols].bitcast(FP8X4),
+                        lhsT_scale=scales[:, cols],
+                        rhs=c_codes[:].bitcast(FP8X4),
+                        rhs_scale=c_scales[:],
+                        start=True,
+                        stop=True,
+                    )
+                pos[g].append(po)
+
+        def store(g):
+            ob = obp.tile([P, GROUP, PO], F32, tag="ob", name="ob%d" % g)
+            for h, po in enumerate(pos[g]):
+                nc.scalar.copy(out=ob[:, 2 * h : 2 * h + 2, :], in_=po[:])
+            nc.sync.dma_start(out=out_v[:, g * GROUP : (g + 1) * GROUP, :], in_=ob[:])
+
+        NPAIR = NT // 2
+        with tc.manual_schedule():
+            for pr in range(NPAIR + 3):
+                pair = [i for i in (2 * pr, 2 * pr + 1) if i < NT]
+                if pr % 2 == 0 and 0 <= (pr - 4) // 2 < NG:
+                    multiply((pr - 4) // 2)
+                if 0 <= 2 * pr - 3 < NT:
+                    expo(2 * pr - 3)
+                for i in pair:
+                    dve_start(i)
+                for i in pair:
+                    dve_step(i, DVE_DIMS[0])
+                if pr % 2 == 1 and 0 <= (pr - 3) // 2 < NG:
+                    quantise((pr - 3) // 2)
+                for d in DVE_DIMS[1:]:
+                    for i in pair:
+                        dve_step(i, d)
+                for i in pair:
+                    act_terms(i)
+                    pool_terms(i)
+                for i in (2 * pr - 2, 2 * pr - 1):
+                    if 0 <= i < NT:
+                        transposes(i)
+                if 0 <= 2 * pr - 2 < NT:
+                    expo(2 * pr - 2)
+                if pr % 2 == 0 and 0 <= (pr - 4) // 2 < NG:
+                    store((pr - 4) // 2)

@@ -23,7 +23,8 @@ NG = NT // GROUP
 FLOPS = 2 * N * M * PO
 
 DVE_DIMS = (0, 1, 2)
-POOL_DIMS = (3, 4, 5)
+TS_DIMS = (3,)
+POOL_DIMS = (4, 5)
 ACT_DIMS = (6, 7)
 NMAX = 6
 BIG = 3.0e38
@@ -38,7 +39,8 @@ def tile_tmgp_sg_t_kernel(tc, x, design_points, chol_inv, out):
         pop = ctx.enter_context(tc.psum_pool(name="pop", bufs=2))
         accp = ctx.enter_context(tc.tile_pool(name="accp", bufs=6))
         tactp = ctx.enter_context(tc.tile_pool(name="tactp", bufs=12))
-        tpoolp = ctx.enter_context(tc.tile_pool(name="tpoolp", bufs=18))
+        tpoolp = ctx.enter_context(tc.tile_pool(name="tpoolp", bufs=12))
+        tdvep = ctx.enter_context(tc.tile_pool(name="tdvep", bufs=6))
         kgp = ctx.enter_context(tc.tile_pool(name="kgp", bufs=3))
         qp = ctx.enter_context(tc.tile_pool(name="qp", bufs=3))
         obp = ctx.enter_context(tc.tile_pool(name="obp", bufs=3))
@@ -80,11 +82,11 @@ def tile_tmgp_sg_t_kernel(tc, x, design_points, chol_inv, out):
             spread(zres, lambda t, d=d: z2[:, t, d : d + 1])
             zc[d] = zres
         turn = 0
-        for d in POOL_DIMS + ACT_DIMS + (D,):
+        for d in TS_DIMS + POOL_DIMS + ACT_DIMS + (D,):
             tmp = ltp.tile([P, M], F32, tag="lt", name="ztmp%d" % d)
             if d == D:
                 spread(tmp, lambda t: rz[:, t : t + 1])
-            elif d in POOL_DIMS:
+            elif d in TS_DIMS + POOL_DIMS:
                 spread(tmp, lambda t, d=d: z2[:, t, d : d + 1])
             else:
                 spread(tmp, lambda t, d=d: zf[:, t, d : d + 1])
@@ -147,21 +149,31 @@ def tile_tmgp_sg_t_kernel(tc, x, design_points, chol_inv, out):
 
         acc = {}
         tact = {}
+        tdve = {}
         tpool = {}
         lts = {}
         kgs = {}
         qs = {}
         pos = {}
 
-        def dve_start(i):
-            a = accp.tile([P, M], F32, tag="acc", name="acc%d" % i)
-            nc.vector.tensor_scalar(out=a[:], in0=rc[:], scalar1=rho[:, i : i + 1], scalar2=None, op0=ALU.add)
-            acc[i] = a
+        def dve_terms(i):
+            tdve[i] = []
+            for d in TS_DIMS:
+                tt = tdvep.tile([P, M], F32, tag="tdve", name="tdve%d_%d" % (i, d))
+                nc.vector.tensor_scalar(
+                    out=tt[:], in0=zc[d][:], scalar1=x2[:, i, d : d + 1], scalar2=rho[:, i : i + 1],
+                    op0=ALU.max, op1=ALU.add,
+                )
+                tdve[i].append(tt)
 
         def dve_step(i, d):
-            a = acc[i]
+            if d == DVE_DIMS[0]:
+                acc[i] = accp.tile([P, M], F32, tag="acc", name="acc%d" % i)
+                prev = rc
+            else:
+                prev = acc[i]
             nc.vector.scalar_tensor_tensor(
-                out=a[:], in0=zc[d][:], scalar=x2[:, i, d : d + 1], in1=a[:], op0=ALU.max, op1=ALU.add
+                out=acc[i][:], in0=zc[d][:], scalar=x2[:, i, d : d + 1], in1=prev[:], op0=ALU.max, op1=ALU.add
             )
 
         def act_terms(i):
@@ -182,7 +194,7 @@ def tile_tmgp_sg_t_kernel(tc, x, design_points, chol_inv, out):
 
         def transposes(i):
             lt = ltp.tile([P, M], F32, tag="lt", name="lt%d" % i)
-            srcs = tpool[i] + tact[i] + [acc[i]]
+            srcs = tdve[i] + tpool[i] + tact[i] + [acc[i]]
             for t in range(PACK):
                 cols = slice(t * P, (t + 1) * P)
                 for j, s in enumerate(srcs):
@@ -251,9 +263,9 @@ def tile_tmgp_sg_t_kernel(tc, x, design_points, chol_inv, out):
                 if 0 <= 2 * pr - 3 < NT:
                     expo(2 * pr - 3)
                 for i in pair:
-                    dve_start(i)
-                for i in pair:
                     dve_step(i, DVE_DIMS[0])
+                for i in pair:
+                    dve_terms(i)
                 if pr % 2 == 1 and 0 <= (pr - 3) // 2 < NG:
                     quantise((pr - 3) // 2)
                 for d in DVE_DIMS[1:]:

@@ -22,8 +22,7 @@ GROUP = 4
 NG = NT // GROUP
 FLOPS = 2 * N * M * PO
 
-DVE_DIMS = (0, 1, 2)
-TS_DIMS = (3,)
+DVE_DIMS = (0, 1, 2, 3)
 POOL_DIMS = (4, 5)
 ACT_DIMS = (6, 7)
 NMAX = 6
@@ -35,12 +34,11 @@ def tile_tmgp_sg_t_kernel(tc, x, design_points, chol_inv, out):
     with ExitStack() as ctx:
         consts = ctx.enter_context(tc.tile_pool(name="consts", bufs=1))
         zbank = ctx.enter_context(tc.psum_pool(name="zbank", bufs=1))
-        ltp = ctx.enter_context(tc.psum_pool(name="ltp", bufs=3))
+        ltp = ctx.enter_context(tc.psum_pool(name="ltp", bufs=2))
         pop = ctx.enter_context(tc.psum_pool(name="pop", bufs=2))
-        accp = ctx.enter_context(tc.tile_pool(name="accp", bufs=6))
+        accp = ctx.enter_context(tc.tile_pool(name="accp", bufs=8))
         tactp = ctx.enter_context(tc.tile_pool(name="tactp", bufs=12))
         tpoolp = ctx.enter_context(tc.tile_pool(name="tpoolp", bufs=12))
-        tdvep = ctx.enter_context(tc.tile_pool(name="tdvep", bufs=6))
         kgp = ctx.enter_context(tc.tile_pool(name="kgp", bufs=3))
         qp = ctx.enter_context(tc.tile_pool(name="qp", bufs=3))
         obp = ctx.enter_context(tc.tile_pool(name="obp", bufs=3))
@@ -82,11 +80,11 @@ def tile_tmgp_sg_t_kernel(tc, x, design_points, chol_inv, out):
             spread(zres, lambda t, d=d: z2[:, t, d : d + 1])
             zc[d] = zres
         turn = 0
-        for d in TS_DIMS + POOL_DIMS + ACT_DIMS + (D,):
+        for d in POOL_DIMS + ACT_DIMS + (D,):
             tmp = ltp.tile([P, M], F32, tag="lt", name="ztmp%d" % d)
             if d == D:
                 spread(tmp, lambda t: rz[:, t : t + 1])
-            elif d in TS_DIMS + POOL_DIMS:
+            elif d in POOL_DIMS:
                 spread(tmp, lambda t, d=d: z2[:, t, d : d + 1])
             else:
                 spread(tmp, lambda t, d=d: zf[:, t, d : d + 1])
@@ -149,31 +147,24 @@ def tile_tmgp_sg_t_kernel(tc, x, design_points, chol_inv, out):
 
         acc = {}
         tact = {}
-        tdve = {}
         tpool = {}
         lts = {}
         kgs = {}
         qs = {}
         pos = {}
 
-        def dve_terms(i):
-            tdve[i] = []
-            for d in TS_DIMS:
-                tt = tdvep.tile([P, M], F32, tag="tdve", name="tdve%d_%d" % (i, d))
-                nc.vector.tensor_scalar(
-                    out=tt[:], in0=zc[d][:], scalar1=x2[:, i, d : d + 1], scalar2=rho[:, i : i + 1],
-                    op0=ALU.max, op1=ALU.add,
+        def seed(i):
+            acc[i] = accp.tile([P, M], F32, tag="acc", name="acc%d" % i)
+            if i % 2 == 0:
+                nc.scalar.activation(out=acc[i][:], in_=rc[:], func=ACTF.Identity, bias=rho[:, i : i + 1], scale=1.0)
+            else:
+                nc.gpsimd.tensor_scalar(
+                    out=acc[i][:], in0=rc[:], scalar1=1.0, scalar2=rho[:, i : i + 1], op0=ALU.mult, op1=ALU.add
                 )
-                tdve[i].append(tt)
 
         def dve_step(i, d):
-            if d == DVE_DIMS[0]:
-                acc[i] = accp.tile([P, M], F32, tag="acc", name="acc%d" % i)
-                prev = rc
-            else:
-                prev = acc[i]
             nc.vector.scalar_tensor_tensor(
-                out=acc[i][:], in0=zc[d][:], scalar=x2[:, i, d : d + 1], in1=prev[:], op0=ALU.max, op1=ALU.add
+                out=acc[i][:], in0=zc[d][:], scalar=x2[:, i, d : d + 1], in1=acc[i][:], op0=ALU.max, op1=ALU.add
             )
 
         def act_terms(i):
@@ -194,7 +185,7 @@ def tile_tmgp_sg_t_kernel(tc, x, design_points, chol_inv, out):
 
         def transposes(i):
             lt = ltp.tile([P, M], F32, tag="lt", name="lt%d" % i)
-            srcs = tdve[i] + tpool[i] + tact[i] + [acc[i]]
+            srcs = tpool[i] + tact[i] + [acc[i]]
             for t in range(PACK):
                 cols = slice(t * P, (t + 1) * P)
                 for j, s in enumerate(srcs):
@@ -256,6 +247,8 @@ def tile_tmgp_sg_t_kernel(tc, x, design_points, chol_inv, out):
 
         NPAIR = NT // 2
         with tc.manual_schedule():
+            seed(0)
+            seed(1)
             for pr in range(NPAIR + 3):
                 pair = [i for i in (2 * pr, 2 * pr + 1) if i < NT]
                 if pr % 2 == 0 and 0 <= (pr - 4) // 2 < NG:
@@ -264,8 +257,6 @@ def tile_tmgp_sg_t_kernel(tc, x, design_points, chol_inv, out):
                     expo(2 * pr - 3)
                 for i in pair:
                     dve_step(i, DVE_DIMS[0])
-                for i in pair:
-                    dve_terms(i)
                 if pr % 2 == 1 and 0 <= (pr - 3) // 2 < NG:
                     quantise((pr - 3) // 2)
                 for d in DVE_DIMS[1:]:
@@ -274,6 +265,9 @@ def tile_tmgp_sg_t_kernel(tc, x, design_points, chol_inv, out):
                 for i in pair:
                     act_terms(i)
                     pool_terms(i)
+                for i in pair:
+                    if i + 2 < NT:
+                        seed(i + 2)
                 for i in (2 * pr - 2, 2 * pr - 1):
                     if 0 <= i < NT:
                         transposes(i)

@@ -1,8 +1,6 @@
 from contextlib import ExitStack
 
-import concourse.bass as bass
 import concourse.mybir as mybir
-import concourse.tile as tile
 from concourse.masks import make_identity
 
 F32 = mybir.dt.float32
@@ -20,6 +18,7 @@ NT = N // P
 PACK = 4
 GROUP = 4
 NG = NT // GROUP
+NPAIR = NT // 2
 FLOPS = 2 * N * M * PO
 
 DVE_DIMS = (0, 1, 2, 3)
@@ -34,7 +33,7 @@ def tile_tmgp_sg_t_kernel(tc, x, design_points, chol_inv, out):
     with ExitStack() as ctx:
         consts = ctx.enter_context(tc.tile_pool(name="consts", bufs=1))
         zbank = ctx.enter_context(tc.psum_pool(name="zbank", bufs=1))
-        ltp = ctx.enter_context(tc.psum_pool(name="ltp", bufs=2))
+        ltp = ctx.enter_context(tc.psum_pool(name="ltp", bufs=4))
         pop = ctx.enter_context(tc.psum_pool(name="pop", bufs=2))
         accp = ctx.enter_context(tc.tile_pool(name="accp", bufs=8))
         tactp = ctx.enter_context(tc.tile_pool(name="tactp", bufs=12))
@@ -52,6 +51,8 @@ def tile_tmgp_sg_t_kernel(tc, x, design_points, chol_inv, out):
 
         ident = consts.tile([P, P], F32)
         make_identity(nc, ident[:])
+        identb = consts.tile([P, P], BF16)
+        make_identity(nc, identb[:])
 
         warm = consts.tile([P, 1], F32)
         nc.vector.memset(warm[:], 0.0)
@@ -61,40 +62,44 @@ def tile_tmgp_sg_t_kernel(tc, x, design_points, chol_inv, out):
         nc.vector.tensor_copy(out=zf[:], in_=z_sb[:])
         z2 = consts.tile([P, PACK, D], F32)
         nc.vector.tensor_scalar(out=z2[:], in0=zf[:], scalar1=2.0, scalar2=None, op0=ALU.mult)
+        z2b = consts.tile([P, PACK, D], BF16)
+        nc.vector.tensor_scalar(out=z2b[:], in0=z_sb[:], scalar1=2.0, scalar2=None, op0=ALU.mult)
         zsum = consts.tile([P, PACK], F32)
         nc.vector.tensor_reduce(out=zsum[:], in_=zf[:, :, 0:NMAX], axis=AX.X, op=ALU.add)
         rz = consts.tile([P, PACK], F32)
         nc.vector.tensor_scalar(out=rz[:], in0=zsum[:], scalar1=-1.0, scalar2=None, op0=ALU.mult)
 
-        def spread(bank, column_of):
+        def spread(bank, column_of, identity):
             for t in range(PACK):
                 nc.tensor.transpose(
                     out=bank[:, t * P : (t + 1) * P],
                     in_=column_of(t).to_broadcast([P, P]),
-                    identity=ident[:],
+                    identity=identity[:],
                 )
 
         zc = {}
-        for d in DVE_DIMS:
-            zres = zbank.tile([P, M], F32, name="zres%d" % d)
-            spread(zres, lambda t, d=d: z2[:, t, d : d + 1])
-            zc[d] = zres
+        for h in range(len(DVE_DIMS) // 2):
+            zres = zbank.tile([P, 2, M], BF16, name="zres%d" % h)
+            for e in range(2):
+                d = DVE_DIMS[2 * h + e]
+                spread(zres[:, e, :], lambda t, d=d: z2b[:, t, d : d + 1], identb)
+                zc[d] = zres[:, e, :]
         turn = 0
         for d in POOL_DIMS + ACT_DIMS + (D,):
             tmp = ltp.tile([P, M], F32, tag="lt", name="ztmp%d" % d)
             if d == D:
-                spread(tmp, lambda t: rz[:, t : t + 1])
+                spread(tmp, lambda t: rz[:, t : t + 1], ident)
             elif d in POOL_DIMS:
-                spread(tmp, lambda t, d=d: z2[:, t, d : d + 1])
+                spread(tmp, lambda t, d=d: z2[:, t, d : d + 1], ident)
             else:
-                spread(tmp, lambda t, d=d: zf[:, t, d : d + 1])
+                spread(tmp, lambda t, d=d: zf[:, t, d : d + 1], ident)
             zs = consts.tile([P, M], F32, name="zs%d" % d)
             if turn % 2 == 0:
                 nc.scalar.copy(out=zs[:], in_=tmp[:])
             else:
                 nc.vector.tensor_copy(out=zs[:], in_=tmp[:])
             turn += 1
-            zc[d] = zs
+            zc[d] = zs[:]
         rc = zc[D]
 
         cg = consts.tile([P, PO, PACK], BF16, align_bytes=64)
@@ -156,22 +161,22 @@ def tile_tmgp_sg_t_kernel(tc, x, design_points, chol_inv, out):
         def seed(i):
             acc[i] = accp.tile([P, M], F32, tag="acc", name="acc%d" % i)
             if i % 2 == 0:
-                nc.scalar.activation(out=acc[i][:], in_=rc[:], func=ACTF.Identity, bias=rho[:, i : i + 1], scale=1.0)
+                nc.scalar.activation(out=acc[i][:], in_=rc, func=ACTF.Identity, bias=rho[:, i : i + 1], scale=1.0)
             else:
                 nc.gpsimd.tensor_scalar(
-                    out=acc[i][:], in0=rc[:], scalar1=1.0, scalar2=rho[:, i : i + 1], op0=ALU.mult, op1=ALU.add
+                    out=acc[i][:], in0=rc, scalar1=1.0, scalar2=rho[:, i : i + 1], op0=ALU.mult, op1=ALU.add
                 )
 
         def dve_step(i, d):
             nc.vector.scalar_tensor_tensor(
-                out=acc[i][:], in0=zc[d][:], scalar=x2[:, i, d : d + 1], in1=acc[i][:], op0=ALU.max, op1=ALU.add
+                out=acc[i][:], in0=zc[d], scalar=x2[:, i, d : d + 1], in1=acc[i][:], op0=ALU.max, op1=ALU.add
             )
 
         def act_terms(i):
             tact[i] = []
             for d in ACT_DIMS:
                 tt = tactp.tile([P, M], F32, tag="tact", name="tact%d_%d" % (i, d))
-                nc.scalar.activation(out=tt[:], in_=zc[d][:], func=ACTF.Abs, bias=nx[:, i, d : d + 1], scale=1.0)
+                nc.scalar.activation(out=tt[:], in_=zc[d], func=ACTF.Abs, bias=nx[:, i, d : d + 1], scale=1.0)
                 tact[i].append(tt)
 
         def pool_terms(i):
@@ -179,7 +184,7 @@ def tile_tmgp_sg_t_kernel(tc, x, design_points, chol_inv, out):
             for d in POOL_DIMS:
                 tt = tpoolp.tile([P, M], F32, tag="tpool", name="tpool%d_%d" % (i, d))
                 nc.gpsimd.tensor_scalar(
-                    out=tt[:], in0=zc[d][:], scalar1=BIG, scalar2=x2[:, i, d : d + 1], op0=ALU.min, op1=ALU.max
+                    out=tt[:], in0=zc[d], scalar1=BIG, scalar2=x2[:, i, d : d + 1], op0=ALU.min, op1=ALU.max
                 )
                 tpool[i].append(tt)
 
@@ -203,10 +208,9 @@ def tile_tmgp_sg_t_kernel(tc, x, design_points, chol_inv, out):
             g, s = divmod(i, GROUP)
             if s == 0:
                 kgs[g] = kgp.tile([P, GROUP, P, PACK], BF16, tag="kg", name="kg%d" % g, align_bytes=64)
-            lt = lts[i]
             nc.scalar.activation(
                 out=kgs[g][:, s, :, :],
-                in_=lt[:].rearrange("p (t n) -> p n t", t=PACK),
+                in_=lts[i][:].rearrange("p (t n) -> p n t", t=PACK),
                 func=ACTF.Exp,
                 scale=-1.0,
             )
@@ -245,33 +249,31 @@ def tile_tmgp_sg_t_kernel(tc, x, design_points, chol_inv, out):
                 nc.scalar.copy(out=ob[:, 2 * h : 2 * h + 2, :], in_=po[:])
             nc.sync.dma_start(out=out_v[:, g * GROUP : (g + 1) * GROUP, :], in_=ob[:])
 
-        NPAIR = NT // 2
+        def tiles_of(pair):
+            return [2 * pair, 2 * pair + 1] if 0 <= pair < NPAIR else []
+
+        def group_at(step):
+            return [step // 2] if step % 2 == 0 and 0 <= step // 2 < NG else []
+
         with tc.manual_schedule():
             seed(0)
             seed(1)
-            for pr in range(NPAIR + 3):
-                pair = [i for i in (2 * pr, 2 * pr + 1) if i < NT]
-                if pr % 2 == 0 and 0 <= (pr - 4) // 2 < NG:
-                    multiply((pr - 4) // 2)
-                if 0 <= 2 * pr - 3 < NT:
-                    expo(2 * pr - 3)
-                for i in pair:
-                    dve_step(i, DVE_DIMS[0])
-                if pr % 2 == 1 and 0 <= (pr - 3) // 2 < NG:
-                    quantise((pr - 3) // 2)
-                for d in DVE_DIMS[1:]:
-                    for i in pair:
+            for pr in range(NPAIR + 5):
+                for g in group_at(pr - 5):
+                    multiply(g)
+                for i in tiles_of(pr - 1):
+                    transposes(i)
+                for i in tiles_of(pr - 2):
+                    expo(i)
+                for g in group_at(pr - 6):
+                    store(g)
+                for g in group_at(pr - 4):
+                    quantise(g)
+                for d in DVE_DIMS:
+                    for i in tiles_of(pr):
                         dve_step(i, d)
-                for i in pair:
+                for i in tiles_of(pr):
                     act_terms(i)
                     pool_terms(i)
-                for i in pair:
-                    if i + 2 < NT:
-                        seed(i + 2)
-                for i in (2 * pr - 2, 2 * pr - 1):
-                    if 0 <= i < NT:
-                        transposes(i)
-                if 0 <= 2 * pr - 2 < NT:
-                    expo(2 * pr - 2)
-                if pr % 2 == 0 and 0 <= (pr - 4) // 2 < NG:
-                    store((pr - 4) // 2)
+                for i in tiles_of(pr + 1):
+                    seed(i)

@@ -26,6 +26,7 @@ POOL_DIMS = (4, 5)
 ACT_DIMS = (6, 7)
 NMAX = 6
 BIG = 3.0e38
+FIRST = 8
 
 
 def tile_tmgp_sg_t_kernel(tc, x, design_points, chol_inv, out):
@@ -53,6 +54,10 @@ def tile_tmgp_sg_t_kernel(tc, x, design_points, chol_inv, out):
         make_identity(nc, ident[:])
         identb = consts.tile([P, P], BF16)
         make_identity(nc, identb[:])
+
+        weight = consts.tile([P, D], F32)
+        nc.vector.memset(weight[:, 0:NMAX], 2.0)
+        nc.vector.memset(weight[:, NMAX:D], -1.0)
 
         warm = consts.tile([P, 1], F32)
         nc.vector.memset(warm[:], 0.0)
@@ -114,11 +119,21 @@ def tile_tmgp_sg_t_kernel(tc, x, design_points, chol_inv, out):
 
         st = consts.tile([P, P], F32)
         nc.vector.memset(st[:], 0.0)
-        xdi = x_sb[:].rearrange("p i d -> p d i")
-        nc.vector.tensor_reduce(out=st[:, 0:D], in_=xdi, axis=AX.X, op=ALU.max)
-        mnp = consts.tile([P, D], F32)
-        nc.vector.tensor_reduce(out=mnp[:], in_=xdi, axis=AX.X, op=ALU.min)
-        nc.vector.tensor_scalar(out=st[:, D : 2 * D], in0=mnp[:], scalar1=-1.0, scalar2=None, op0=ALU.mult)
+        hi_prev, lo_prev = x_sb, x_sb
+        half = NT // 2
+        while half >= 1:
+            hi_next = consts.tile([P, half, D], BF16, name="hi%d" % half)
+            lo_next = consts.tile([P, half, D], BF16, name="lo%d" % half)
+            nc.vector.tensor_tensor(
+                out=hi_next[:], in0=hi_prev[:, 0:half, :], in1=hi_prev[:, half : 2 * half, :], op=ALU.max
+            )
+            nc.vector.tensor_tensor(
+                out=lo_next[:], in0=lo_prev[:, 0:half, :], in1=lo_prev[:, half : 2 * half, :], op=ALU.min
+            )
+            hi_prev, lo_prev = hi_next, lo_next
+            half //= 2
+        nc.vector.tensor_copy(out=st[:, 0:D], in_=hi_prev[:, 0, :])
+        nc.vector.tensor_scalar(out=st[:, D : 2 * D], in0=lo_prev[:, 0, :], scalar1=-1.0, scalar2=None, op0=ALU.mult)
         stT = pop.tile([P, M], F32, tag="po", name="stT")
         nc.tensor.transpose(out=stT[:, 0:P], in_=st[:], identity=ident[:])
         gcol = consts.tile([P, 1], F32)
@@ -131,22 +146,35 @@ def tile_tmgp_sg_t_kernel(tc, x, design_points, chol_inv, out):
         nc.vector.tensor_tensor(out=rng[:], in0=gs[:, 0:D], in1=gs[:, D : 2 * D], op=ALU.add)
         rinv = consts.tile([P, D], F32)
         nc.vector.reciprocal(out=rinv[:], in_=rng[:])
-        r2 = consts.tile([P, D], F32)
-        nc.vector.tensor_scalar(out=r2[:], in0=rinv[:], scalar1=2.0, scalar2=None, op0=ALU.mult)
-        rneg = consts.tile([P, D], F32)
-        nc.vector.tensor_scalar(out=rneg[:], in0=rinv[:], scalar1=-1.0, scalar2=None, op0=ALU.mult)
+        factor = consts.tile([P, D], F32)
+        nc.vector.tensor_tensor(out=factor[:], in0=rinv[:], in1=weight[:], op=ALU.mult)
+        shift = consts.tile([P, D], F32)
+        nc.vector.tensor_tensor(out=shift[:], in0=gs[:, D : 2 * D], in1=factor[:], op=ALU.mult)
 
-        def over_tiles(v):
-            return v.unsqueeze(1).to_broadcast([P, NT, D])
-
-        xm = consts.tile([P, NT, D], F32)
-        nc.vector.tensor_tensor(out=xm[:], in0=x_sb[:], in1=over_tiles(gs[:, D : 2 * D]), op=ALU.add)
-        x2 = consts.tile([P, NT, D], F32)
-        nc.vector.tensor_tensor(out=x2[:], in0=xm[:], in1=over_tiles(r2[:]), op=ALU.mult)
-        nx = consts.tile([P, NT, D], F32)
-        nc.vector.tensor_tensor(out=nx[:], in0=xm[:], in1=over_tiles(rneg[:]), op=ALU.mult)
+        xv = consts.tile([P, D, NT], F32)
+        first = xv[:, :, 0:FIRST]
+        nc.vector.tensor_tensor(
+            out=first, in0=x_sb[:, 0:FIRST, :].rearrange("p i d -> p d i"),
+            in1=factor[:].unsqueeze(2).to_broadcast([P, D, FIRST]), op=ALU.mult,
+        )
+        nc.vector.tensor_tensor(
+            out=first, in0=first, in1=shift[:].unsqueeze(2).to_broadcast([P, D, FIRST]), op=ALU.add
+        )
+        for d in range(D):
+            nc.scalar.activation(
+                out=xv[:, d, FIRST:NT], in_=x_sb[:, FIRST:NT, d], func=ACTF.Identity,
+                scale=factor[:, d : d + 1], bias=shift[:, d : d + 1],
+            )
         rho = consts.tile([P, NT], F32)
-        nc.vector.tensor_reduce(out=rho[:], in_=nx[:, :, 0:NMAX], axis=AX.X, op=ALU.add)
+        xsum = consts.tile([P, NT], F32)
+
+        def make_rho(lo, hi):
+            nc.vector.tensor_reduce(
+                out=xsum[:, lo:hi], in_=xv[:, 0:NMAX, lo:hi].rearrange("p d i -> p i d"), axis=AX.X, op=ALU.add
+            )
+            nc.vector.tensor_scalar(out=rho[:, lo:hi], in0=xsum[:, lo:hi], scalar1=-0.5, scalar2=None, op0=ALU.mult)
+
+        make_rho(0, FIRST)
 
         out_v = out.rearrange("(p i) w -> p i w", p=P)
 
@@ -169,14 +197,14 @@ def tile_tmgp_sg_t_kernel(tc, x, design_points, chol_inv, out):
 
         def dve_step(i, d):
             nc.vector.scalar_tensor_tensor(
-                out=acc[i][:], in0=zc[d], scalar=x2[:, i, d : d + 1], in1=acc[i][:], op0=ALU.max, op1=ALU.add
+                out=acc[i][:], in0=zc[d], scalar=xv[:, d, i : i + 1], in1=acc[i][:], op0=ALU.max, op1=ALU.add
             )
 
         def act_terms(i):
             tact[i] = []
             for d in ACT_DIMS:
                 tt = tactp.tile([P, M], F32, tag="tact", name="tact%d_%d" % (i, d))
-                nc.scalar.activation(out=tt[:], in_=zc[d], func=ACTF.Abs, bias=nx[:, i, d : d + 1], scale=1.0)
+                nc.scalar.activation(out=tt[:], in_=zc[d], func=ACTF.Abs, bias=xv[:, d, i : i + 1], scale=1.0)
                 tact[i].append(tt)
 
         def pool_terms(i):
@@ -184,7 +212,7 @@ def tile_tmgp_sg_t_kernel(tc, x, design_points, chol_inv, out):
             for d in POOL_DIMS:
                 tt = tpoolp.tile([P, M], F32, tag="tpool", name="tpool%d_%d" % (i, d))
                 nc.gpsimd.tensor_scalar(
-                    out=tt[:], in0=zc[d], scalar1=BIG, scalar2=x2[:, i, d : d + 1], op0=ALU.min, op1=ALU.max
+                    out=tt[:], in0=zc[d], scalar1=BIG, scalar2=xv[:, d, i : i + 1], op0=ALU.min, op1=ALU.max
                 )
                 tpool[i].append(tt)
 
@@ -272,6 +300,8 @@ def tile_tmgp_sg_t_kernel(tc, x, design_points, chol_inv, out):
                 for d in DVE_DIMS:
                     for i in tiles_of(pr):
                         dve_step(i, d)
+                if pr == 0:
+                    make_rho(FIRST, NT)
                 for i in tiles_of(pr):
                     act_terms(i)
                     pool_terms(i)

@@ -26,6 +26,8 @@ POOL_DIMS = (4, 5)
 ACT_DIMS = (6, 7)
 NMAX = 6
 BIG = 3.0e38
+GIVE_EVERY = 8
+POOL_SEED_EVERY = 2
 FIRST = 8
 
 
@@ -38,7 +40,7 @@ def tile_tmgp_sg_t_kernel(tc, x, design_points, chol_inv, out):
         pop = ctx.enter_context(tc.psum_pool(name="pop", bufs=2))
         accp = ctx.enter_context(tc.tile_pool(name="accp", bufs=8))
         tactp = ctx.enter_context(tc.tile_pool(name="tactp", bufs=12))
-        tpoolp = ctx.enter_context(tc.tile_pool(name="tpoolp", bufs=12))
+        tpoolp = ctx.enter_context(tc.tile_pool(name="tpoolp", bufs=14))
         kgp = ctx.enter_context(tc.tile_pool(name="kgp", bufs=3))
         qp = ctx.enter_context(tc.tile_pool(name="qp", bufs=3))
         obp = ctx.enter_context(tc.tile_pool(name="obp", bufs=3))
@@ -83,18 +85,19 @@ def tile_tmgp_sg_t_kernel(tc, x, design_points, chol_inv, out):
                 )
 
         zc = {}
+        zp = {}
         for h in range(len(DVE_DIMS) // 2):
             zres = zbank.tile([P, 2, M], BF16, name="zres%d" % h)
             for e in range(2):
                 d = DVE_DIMS[2 * h + e]
                 spread(zres[:, e, :], lambda t, d=d: z2b[:, t, d : d + 1], identb)
-                zc[d] = zres[:, e, :]
+                zp[d] = zres[:, e, :]
         turn = 0
-        for d in POOL_DIMS + ACT_DIMS + (D,):
+        for d in DVE_DIMS[3:4] + POOL_DIMS + ACT_DIMS + (D,):
             tmp = ltp.tile([P, M], F32, tag="lt", name="ztmp%d" % d)
             if d == D:
                 spread(tmp, lambda t: rz[:, t : t + 1], ident)
-            elif d in POOL_DIMS:
+            elif d < NMAX:
                 spread(tmp, lambda t, d=d: z2[:, t, d : d + 1], ident)
             else:
                 spread(tmp, lambda t, d=d: zf[:, t, d : d + 1], ident)
@@ -186,9 +189,12 @@ def tile_tmgp_sg_t_kernel(tc, x, design_points, chol_inv, out):
         qs = {}
         pos = {}
 
+        def gives(i):
+            return i % GIVE_EVERY == GIVE_EVERY - 2
+
         def seed(i):
             acc[i] = accp.tile([P, M], F32, tag="acc", name="acc%d" % i)
-            if i % 2 == 0:
+            if i % POOL_SEED_EVERY != 1:
                 nc.scalar.activation(out=acc[i][:], in_=rc, func=ACTF.Identity, bias=rho[:, i : i + 1], scale=1.0)
             else:
                 nc.gpsimd.tensor_scalar(
@@ -197,7 +203,7 @@ def tile_tmgp_sg_t_kernel(tc, x, design_points, chol_inv, out):
 
         def dve_step(i, d):
             nc.vector.scalar_tensor_tensor(
-                out=acc[i][:], in0=zc[d], scalar=xv[:, d, i : i + 1], in1=acc[i][:], op0=ALU.max, op1=ALU.add
+                out=acc[i][:], in0=zp[d], scalar=xv[:, d, i : i + 1], in1=acc[i][:], op0=ALU.max, op1=ALU.add
             )
 
         def act_terms(i):
@@ -209,7 +215,7 @@ def tile_tmgp_sg_t_kernel(tc, x, design_points, chol_inv, out):
 
         def pool_terms(i):
             tpool[i] = []
-            for d in POOL_DIMS:
+            for d in (DVE_DIMS[3:4] + POOL_DIMS if gives(i) else POOL_DIMS):
                 tt = tpoolp.tile([P, M], F32, tag="tpool", name="tpool%d_%d" % (i, d))
                 nc.gpsimd.tensor_scalar(
                     out=tt[:], in0=zc[d], scalar1=BIG, scalar2=xv[:, d, i : i + 1], op0=ALU.min, op1=ALU.max
@@ -298,8 +304,9 @@ def tile_tmgp_sg_t_kernel(tc, x, design_points, chol_inv, out):
                 for g in group_at(pr - 4):
                     quantise(g)
                 for d in DVE_DIMS:
-                    for i in tiles_of(pr):
-                        dve_step(i, d)
+                    for i in reversed(tiles_of(pr)):
+                        if d != DVE_DIMS[3] or not gives(i):
+                            dve_step(i, d)
                 if pr == 0:
                     make_rho(FIRST, NT)
                 for i in tiles_of(pr):

@@ -26,7 +26,7 @@ POOL_DIMS = (4, 5)
 ACT_DIMS = (6, 7)
 NMAX = 6
 BIG = 3.0e38
-GIVE_EVERY = 8
+GIVE_EVERY = 16
 POOL_SEED_EVERY = 2
 FIRST = 8
 

@@ -26,8 +26,10 @@ POOL_DIMS = (4, 5)
 ACT_DIMS = (6, 7)
 NMAX = 6
 BIG = 3.0e38
-GIVE_EVERY = 16
-POOL_SEED_EVERY = 2
+STEP_DIMS = (0, 3, 1, 2)
+RHO_DIM = 3
+GIVE_DIM = 2
+GIVE_EVERY = 4
 FIRST = 8
 
 
@@ -39,38 +41,66 @@ def tile_tmgp_sg_t_kernel(tc, x, design_points, chol_inv, out):
         ltp = ctx.enter_context(tc.psum_pool(name="ltp", bufs=4))
         pop = ctx.enter_context(tc.psum_pool(name="pop", bufs=2))
         accp = ctx.enter_context(tc.tile_pool(name="accp", bufs=8))
+        tvp = ctx.enter_context(tc.tile_pool(name="tvp", bufs=8))
         tactp = ctx.enter_context(tc.tile_pool(name="tactp", bufs=12))
         tpoolp = ctx.enter_context(tc.tile_pool(name="tpoolp", bufs=14))
         kgp = ctx.enter_context(tc.tile_pool(name="kgp", bufs=3))
         qp = ctx.enter_context(tc.tile_pool(name="qp", bufs=3))
         obp = ctx.enter_context(tc.tile_pool(name="obp", bufs=3))
+        ctx.enter_context(tc.manual_schedule())
 
         z_sb = consts.tile([P, PACK, D], BF16)
-        nc.sync.dma_start(out=z_sb[:], in_=design_points.rearrange("(p t) d -> p t d", t=PACK))
+        nc.scalar.dma_start(out=z_sb[:], in_=design_points.rearrange("(p t) d -> p t d", t=PACK))
         x_sb = consts.tile([P, NT, D], BF16)
         nc.sync.dma_start(out=x_sb[:], in_=x.rearrange("(p i) d -> p i d", p=P))
         c_sb = consts.tile([P, PACK, PO], BF16)
         nc.sync.dma_start(out=c_sb[:], in_=chol_inv.rearrange("(p t) w -> p t w", t=PACK))
 
-        ident = consts.tile([P, P], F32)
-        make_identity(nc, ident[:])
         identb = consts.tile([P, P], BF16)
         make_identity(nc, identb[:])
-
-        weight = consts.tile([P, D], F32)
-        nc.vector.memset(weight[:, 0:NMAX], 2.0)
-        nc.vector.memset(weight[:, NMAX:D], -1.0)
+        ident = consts.tile([P, P], F32)
+        make_identity(nc, ident[:])
 
         warm = consts.tile([P, 1], F32)
         nc.vector.memset(warm[:], 0.0)
         nc.scalar.activation(out=warm[:], in_=warm[:], func=ACTF.Exp)
 
-        zf = consts.tile([P, PACK, D], F32)
-        nc.vector.tensor_copy(out=zf[:], in_=z_sb[:])
-        z2 = consts.tile([P, PACK, D], F32)
-        nc.vector.tensor_scalar(out=z2[:], in0=zf[:], scalar1=2.0, scalar2=None, op0=ALU.mult)
+        st = consts.tile([P, P], F32)
+        nc.vector.memset(st[:], 0.0)
+        sel = consts.tile([P, 3 * D], F32)
+        nc.vector.tensor_copy(out=sel[:, 0 : 2 * D], in_=ident[:, 0 : 2 * D])
+        nc.vector.tensor_tensor(out=sel[:, 2 * D : 3 * D], in0=ident[:, 0:D], in1=ident[:, D : 2 * D], op=ALU.add)
+        nc.vector.tensor_scalar(
+            out=sel[:, 2 * D : 2 * D + NMAX], in0=sel[:, 2 * D : 2 * D + NMAX], scalar1=0.5, scalar2=None, op0=ALU.mult
+        )
+        nc.vector.tensor_scalar(
+            out=sel[:, 2 * D + NMAX : 3 * D], in0=sel[:, 2 * D + NMAX : 3 * D], scalar1=-1.0, scalar2=None, op0=ALU.mult
+        )
+
+        hi_prev, lo_prev = x_sb, x_sb
+        half = NT // 2
+        while half >= 16:
+            hi_next = consts.tile([P, half, D], BF16, name="hi%d" % half)
+            lo_next = consts.tile([P, half, D], BF16, name="lo%d" % half)
+            nc.vector.tensor_tensor(
+                out=hi_next[:], in0=hi_prev[:, 0:half, :], in1=hi_prev[:, half : 2 * half, :], op=ALU.max
+            )
+            nc.vector.tensor_tensor(
+                out=lo_next[:], in0=lo_prev[:, 0:half, :], in1=lo_prev[:, half : 2 * half, :], op=ALU.min
+            )
+            hi_prev, lo_prev = hi_next, lo_next
+            half //= 2
+        low = consts.tile([P, D], F32)
+        nc.vector.tensor_reduce(out=low[:], in_=lo_prev[:].rearrange("p i d -> p d i"), axis=AX.X, op=ALU.min)
+        nc.vector.tensor_reduce(out=st[:, 0:D], in_=hi_prev[:].rearrange("p i d -> p d i"), axis=AX.X, op=ALU.max)
+        nc.vector.tensor_scalar(out=st[:, D : 2 * D], in0=low[:], scalar1=-1.0, scalar2=None, op0=ALU.mult)
+
         z2b = consts.tile([P, PACK, D], BF16)
-        nc.vector.tensor_scalar(out=z2b[:], in0=z_sb[:], scalar1=2.0, scalar2=None, op0=ALU.mult)
+        nc.scalar.activation(out=z2b[:], in_=z_sb[:], func=ACTF.Copy, scale=2.0)
+        zf = consts.tile([P, PACK, D], F32)
+        nc.scalar.activation(out=zf[:], in_=z_sb[:], func=ACTF.Copy)
+        z2 = consts.tile([P, PACK, D], F32)
+        nc.scalar.activation(out=z2[:], in_=z_sb[:], func=ACTF.Copy, scale=2.0)
         zsum = consts.tile([P, PACK], F32)
         nc.vector.tensor_reduce(out=zsum[:], in_=zf[:, :, 0:NMAX], axis=AX.X, op=ALU.add)
         rz = consts.tile([P, PACK], F32)
@@ -84,7 +114,6 @@ def tile_tmgp_sg_t_kernel(tc, x, design_points, chol_inv, out):
                     identity=identity[:],
                 )
 
-        zc = {}
         zp = {}
         for h in range(len(DVE_DIMS) // 2):
             zres = zbank.tile([P, 2, M], BF16, name="zres%d" % h)
@@ -92,68 +121,39 @@ def tile_tmgp_sg_t_kernel(tc, x, design_points, chol_inv, out):
                 d = DVE_DIMS[2 * h + e]
                 spread(zres[:, e, :], lambda t, d=d: z2b[:, t, d : d + 1], identb)
                 zp[d] = zres[:, e, :]
-        turn = 0
-        for d in DVE_DIMS[3:4] + POOL_DIMS + ACT_DIMS + (D,):
+
+        zc = {}
+
+        def constant(d):
             tmp = ltp.tile([P, M], F32, tag="lt", name="ztmp%d" % d)
             if d == D:
                 spread(tmp, lambda t: rz[:, t : t + 1], ident)
             elif d < NMAX:
-                spread(tmp, lambda t, d=d: z2[:, t, d : d + 1], ident)
+                spread(tmp, lambda t: z2[:, t, d : d + 1], ident)
             else:
-                spread(tmp, lambda t, d=d: zf[:, t, d : d + 1], ident)
+                spread(tmp, lambda t: zf[:, t, d : d + 1], ident)
             zs = consts.tile([P, M], F32, name="zs%d" % d)
-            if turn % 2 == 0:
-                nc.scalar.copy(out=zs[:], in_=tmp[:])
-            else:
-                nc.vector.tensor_copy(out=zs[:], in_=tmp[:])
-            turn += 1
+            nc.scalar.copy(out=zs[:], in_=tmp[:])
             zc[d] = zs[:]
-        rc = zc[D]
 
-        cg = consts.tile([P, PO, PACK], BF16, align_bytes=64)
-        nc.vector.tensor_copy(out=cg[:], in_=c_sb[:].rearrange("p t w -> p w t"))
-        c_codes = consts.tile([P, PO], U32, align_bytes=64)
-        c_scales = consts.tile([P, PO], U8, align_bytes=64)
-        nc.vector.quantize_mx(
-            out=c_codes[:].bitcast(FP8X4),
-            scales=c_scales[:],
-            in_=cg[:].rearrange("p w t -> p (w t)"),
-        )
-
-        st = consts.tile([P, P], F32)
-        nc.vector.memset(st[:], 0.0)
-        hi_prev, lo_prev = x_sb, x_sb
-        half = NT // 2
-        while half >= 1:
-            hi_next = consts.tile([P, half, D], BF16, name="hi%d" % half)
-            lo_next = consts.tile([P, half, D], BF16, name="lo%d" % half)
-            nc.vector.tensor_tensor(
-                out=hi_next[:], in0=hi_prev[:, 0:half, :], in1=hi_prev[:, half : 2 * half, :], op=ALU.max
-            )
-            nc.vector.tensor_tensor(
-                out=lo_next[:], in0=lo_prev[:, 0:half, :], in1=lo_prev[:, half : 2 * half, :], op=ALU.min
-            )
-            hi_prev, lo_prev = hi_next, lo_next
-            half //= 2
-        nc.vector.tensor_copy(out=st[:, 0:D], in_=hi_prev[:, 0, :])
-        nc.vector.tensor_scalar(out=st[:, D : 2 * D], in0=lo_prev[:, 0, :], scalar1=-1.0, scalar2=None, op0=ALU.mult)
+        constant(ACT_DIMS[0])
         stT = pop.tile([P, M], F32, tag="po", name="stT")
         nc.tensor.transpose(out=stT[:, 0:P], in_=st[:], identity=ident[:])
         gcol = consts.tile([P, 1], F32)
         nc.vector.tensor_reduce(out=gcol[:], in_=stT[:, 0:P], axis=AX.X, op=ALU.max)
+        constant(ACT_DIMS[1])
         gb = pop.tile([P, M], F32, tag="po", name="gb")
-        nc.tensor.transpose(out=gb[:, 0:P], in_=gcol[:, 0:1].to_broadcast([P, P]), identity=ident[:])
-        gs = consts.tile([P, 2 * D], F32)
-        nc.vector.tensor_copy(out=gs[:], in_=gb[:, 0 : 2 * D])
-        rng = consts.tile([P, D], F32)
-        nc.vector.tensor_tensor(out=rng[:], in0=gs[:, 0:D], in1=gs[:, D : 2 * D], op=ALU.add)
-        rinv = consts.tile([P, D], F32)
-        nc.vector.reciprocal(out=rinv[:], in_=rng[:])
-        factor = consts.tile([P, D], F32)
-        nc.vector.tensor_tensor(out=factor[:], in0=rinv[:], in1=weight[:], op=ALU.mult)
-        shift = consts.tile([P, D], F32)
-        nc.vector.tensor_tensor(out=shift[:], in0=gs[:, D : 2 * D], in1=factor[:], op=ALU.mult)
+        nc.tensor.matmul(
+            out=gb[:, 0 : 3 * D], lhsT=gcol[:, 0:1].to_broadcast([P, P]), rhs=sel[:], start=True, stop=True
+        )
+        for d in (D,) + POOL_DIMS + (GIVE_DIM,):
+            constant(d)
+        rc = zc[D]
 
+        factor = consts.tile([P, D], F32)
+        nc.vector.reciprocal(out=factor[:], in_=gb[:, 2 * D : 3 * D])
+        shift = consts.tile([P, D], F32)
+        nc.vector.tensor_tensor(out=shift[:], in0=gb[:, D : 2 * D], in1=factor[:], op=ALU.mult)
         xv = consts.tile([P, D, NT], F32)
         first = xv[:, :, 0:FIRST]
         nc.vector.tensor_tensor(
@@ -163,13 +163,15 @@ def tile_tmgp_sg_t_kernel(tc, x, design_points, chol_inv, out):
         nc.vector.tensor_tensor(
             out=first, in0=first, in1=shift[:].unsqueeze(2).to_broadcast([P, D, FIRST]), op=ALU.add
         )
-        for d in range(D):
-            nc.scalar.activation(
-                out=xv[:, d, FIRST:NT], in_=x_sb[:, FIRST:NT, d], func=ACTF.Identity,
-                scale=factor[:, d : d + 1], bias=shift[:, d : d + 1],
-            )
         rho = consts.tile([P, NT], F32)
         xsum = consts.tile([P, NT], F32)
+
+        def make_rest_of_xv():
+            for d in range(D):
+                nc.scalar.activation(
+                    out=xv[:, d, FIRST:NT], in_=x_sb[:, FIRST:NT, d], func=ACTF.Identity,
+                    scale=factor[:, d : d + 1], bias=shift[:, d : d + 1],
+                )
 
         def make_rho(lo, hi):
             nc.vector.tensor_reduce(
@@ -177,11 +179,24 @@ def tile_tmgp_sg_t_kernel(tc, x, design_points, chol_inv, out):
             )
             nc.vector.tensor_scalar(out=rho[:, lo:hi], in0=xsum[:, lo:hi], scalar1=-0.5, scalar2=None, op0=ALU.mult)
 
-        make_rho(0, FIRST)
+        cg = consts.tile([P, PO, PACK], BF16, align_bytes=64)
+        c_codes = consts.tile([P, PO], U32, align_bytes=64)
+        c_scales = consts.tile([P, PO], U8, align_bytes=64)
+
+        def interleave_c():
+            nc.scalar.copy(out=cg[:], in_=c_sb[:].rearrange("p t w -> p w t"))
+
+        def quantise_c():
+            nc.vector.quantize_mx(
+                out=c_codes[:].bitcast(FP8X4),
+                scales=c_scales[:],
+                in_=cg[:].rearrange("p w t -> p (w t)"),
+            )
 
         out_v = out.rearrange("(p i) w -> p i w", p=P)
 
         acc = {}
+        tv = {}
         tact = {}
         tpool = {}
         lts = {}
@@ -192,18 +207,21 @@ def tile_tmgp_sg_t_kernel(tc, x, design_points, chol_inv, out):
         def gives(i):
             return i % GIVE_EVERY == GIVE_EVERY - 2
 
-        def seed(i):
-            acc[i] = accp.tile([P, M], F32, tag="acc", name="acc%d" % i)
-            if i % POOL_SEED_EVERY != 1:
-                nc.scalar.activation(out=acc[i][:], in_=rc, func=ACTF.Identity, bias=rho[:, i : i + 1], scale=1.0)
-            else:
-                nc.gpsimd.tensor_scalar(
-                    out=acc[i][:], in0=rc, scalar1=1.0, scalar2=rho[:, i : i + 1], op0=ALU.mult, op1=ALU.add
-                )
-
         def dve_step(i, d):
+            if d == RHO_DIM:
+                tv[i] = tvp.tile([P, M], F32, tag="tv", name="tv%d" % i)
+                nc.vector.tensor_scalar(
+                    out=tv[i][:], in0=zp[d], scalar1=xv[:, d, i : i + 1], scalar2=rho[:, i : i + 1],
+                    op0=ALU.max, op1=ALU.add,
+                )
+                return
+            if d == DVE_DIMS[0]:
+                acc[i] = accp.tile([P, M], F32, tag="acc", name="acc%d" % i)
+                prior = rc
+            else:
+                prior = acc[i][:]
             nc.vector.scalar_tensor_tensor(
-                out=acc[i][:], in0=zp[d], scalar=xv[:, d, i : i + 1], in1=acc[i][:], op0=ALU.max, op1=ALU.add
+                out=acc[i][:], in0=zp[d], scalar=xv[:, d, i : i + 1], in1=prior, op0=ALU.max, op1=ALU.add
             )
 
         def act_terms(i):
@@ -215,7 +233,7 @@ def tile_tmgp_sg_t_kernel(tc, x, design_points, chol_inv, out):
 
         def pool_terms(i):
             tpool[i] = []
-            for d in (DVE_DIMS[3:4] + POOL_DIMS if gives(i) else POOL_DIMS):
+            for d in ((GIVE_DIM,) + POOL_DIMS if gives(i) else POOL_DIMS):
                 tt = tpoolp.tile([P, M], F32, tag="tpool", name="tpool%d_%d" % (i, d))
                 nc.gpsimd.tensor_scalar(
                     out=tt[:], in0=zc[d], scalar1=BIG, scalar2=xv[:, d, i : i + 1], op0=ALU.min, op1=ALU.max
@@ -224,7 +242,7 @@ def tile_tmgp_sg_t_kernel(tc, x, design_points, chol_inv, out):
 
         def transposes(i):
             lt = ltp.tile([P, M], F32, tag="lt", name="lt%d" % i)
-            srcs = tpool[i] + tact[i] + [acc[i]]
+            srcs = [acc[i], tv[i]] + tpool[i][::-1] + tact[i][::-1]
             for t in range(PACK):
                 cols = slice(t * P, (t + 1) * P)
                 for j, s in enumerate(srcs):
@@ -240,7 +258,7 @@ def tile_tmgp_sg_t_kernel(tc, x, design_points, chol_inv, out):
 
         def expo(i):
             g, s = divmod(i, GROUP)
-            if s == 0:
+            if g not in kgs:
                 kgs[g] = kgp.tile([P, GROUP, P, PACK], BF16, tag="kg", name="kg%d" % g, align_bytes=64)
             nc.scalar.activation(
                 out=kgs[g][:, s, :, :],
@@ -289,28 +307,30 @@ def tile_tmgp_sg_t_kernel(tc, x, design_points, chol_inv, out):
         def group_at(step):
             return [step // 2] if step % 2 == 0 and 0 <= step // 2 < NG else []
 
-        with tc.manual_schedule():
-            seed(0)
-            seed(1)
-            for pr in range(NPAIR + 5):
-                for g in group_at(pr - 5):
-                    multiply(g)
-                for i in tiles_of(pr - 1):
-                    transposes(i)
-                for i in tiles_of(pr - 2):
-                    expo(i)
-                for g in group_at(pr - 6):
-                    store(g)
-                for g in group_at(pr - 4):
-                    quantise(g)
-                for d in DVE_DIMS:
-                    for i in reversed(tiles_of(pr)):
-                        if d != DVE_DIMS[3] or not gives(i):
-                            dve_step(i, d)
-                if pr == 0:
-                    make_rho(FIRST, NT)
+        for pr in range(NPAIR + 5):
+            for g in group_at(pr - 5):
+                multiply(g)
+            for i in reversed(tiles_of(pr - 1)):
+                transposes(i)
+            for i in reversed(tiles_of(pr - 2)):
+                expo(i)
+            for g in group_at(pr - 6):
+                store(g)
+            for g in group_at(pr - 4):
+                quantise(g)
+            for d in STEP_DIMS:
                 for i in tiles_of(pr):
-                    act_terms(i)
-                    pool_terms(i)
-                for i in tiles_of(pr + 1):
-                    seed(i)
+                    if d != GIVE_DIM or not gives(i):
+                        dve_step(i, d)
+                if pr == 0 and d == DVE_DIMS[0]:
+                    make_rho(0, FIRST)
+            for i in tiles_of(pr):
+                act_terms(i)
+                pool_terms(i)
+            if pr == 0:
+                make_rest_of_xv()
+            if pr == 1:
+                make_rho(FIRST, NT)
+                interleave_c()
+            if pr == 2:
+                quantise_c()

@@ -240,21 +240,23 @@ def tile_tmgp_sg_t_kernel(tc, x, design_points, chol_inv, out):
                 )
                 tpool[i].append(tt)
 
-        def transposes(i):
-            lt = ltp.tile([P, M], F32, tag="lt", name="lt%d" % i)
-            srcs = [acc[i], tv[i]] + tpool[i][::-1] + tact[i][::-1]
+        def transposes(tiles):
+            srcs = {i: [acc[i], tv[i]] + tpool[i][::-1] + tact[i][::-1] for i in tiles}
+            for i in tiles:
+                lts[i] = ltp.tile([P, M], F32, tag="lt", name="lt%d" % i)
             for t in range(PACK):
                 cols = slice(t * P, (t + 1) * P)
-                for j, s in enumerate(srcs):
-                    nc.tensor.matmul(
-                        out=lt[:, cols],
-                        lhsT=s[:, cols],
-                        rhs=ident[:],
-                        start=(j == 0),
-                        stop=(j == len(srcs) - 1),
-                        is_transpose=True,
-                    )
-            lts[i] = lt
+                for j in range(max(len(srcs[i]) for i in tiles)):
+                    for i in tiles:
+                        if j < len(srcs[i]):
+                            nc.tensor.matmul(
+                                out=lts[i][:, cols],
+                                lhsT=srcs[i][j][:, cols],
+                                rhs=ident[:],
+                                start=(j == 0),
+                                stop=(j == len(srcs[i]) - 1),
+                                is_transpose=True,
+                            )
 
         def expo(i):
             g, s = divmod(i, GROUP)
@@ -310,8 +312,8 @@ def tile_tmgp_sg_t_kernel(tc, x, design_points, chol_inv, out):
         for pr in range(NPAIR + 5):
             for g in group_at(pr - 5):
                 multiply(g)
-            for i in reversed(tiles_of(pr - 1)):
-                transposes(i)
+            if tiles_of(pr - 1):
+                transposes(tiles_of(pr - 1)[::-1])
             for i in reversed(tiles_of(pr - 2)):
                 expo(i)
             for g in group_at(pr - 6):

@@ -27,9 +27,8 @@ ACT_DIMS = (6, 7)
 NMAX = 6
 BIG = 3.0e38
 STEP_DIMS = (0, 3, 1, 2)
-RHO_DIM = 3
-GIVE_DIM = 2
-GIVE_EVERY = 4
+LAST_DIM = 3
+KEEP_EVERY = 8
 FIRST = 8
 
 
@@ -146,7 +145,7 @@ def tile_tmgp_sg_t_kernel(tc, x, design_points, chol_inv, out):
         nc.tensor.matmul(
             out=gb[:, 0 : 3 * D], lhsT=gcol[:, 0:1].to_broadcast([P, P]), rhs=sel[:], start=True, stop=True
         )
-        for d in (D,) + POOL_DIMS + (GIVE_DIM,):
+        for d in (D,) + POOL_DIMS + (LAST_DIM,):
             constant(d)
         rc = zc[D]
 
@@ -205,17 +204,24 @@ def tile_tmgp_sg_t_kernel(tc, x, design_points, chol_inv, out):
         pos = {}
 
         def gives(i):
-            return i % GIVE_EVERY == GIVE_EVERY - 2
+            return seeded(i) and i // 2 % KEEP_EVERY != KEEP_EVERY - 1
+
+        def seeded(i):
+            return i // 2 % 2 == 1
+
+        def seed(i):
+            acc[i] = accp.tile([P, M], F32, tag="acc", name="acc%d" % i)
+            nc.scalar.activation(out=acc[i][:], in_=rc, func=ACTF.Identity, bias=rho[:, i : i + 1], scale=1.0)
 
         def dve_step(i, d):
-            if d == RHO_DIM:
+            if d == LAST_DIM and not seeded(i):
                 tv[i] = tvp.tile([P, M], F32, tag="tv", name="tv%d" % i)
                 nc.vector.tensor_scalar(
                     out=tv[i][:], in0=zp[d], scalar1=xv[:, d, i : i + 1], scalar2=rho[:, i : i + 1],
                     op0=ALU.max, op1=ALU.add,
                 )
                 return
-            if d == DVE_DIMS[0]:
+            if d == DVE_DIMS[0] and not seeded(i):
                 acc[i] = accp.tile([P, M], F32, tag="acc", name="acc%d" % i)
                 prior = rc
             else:
@@ -233,7 +239,7 @@ def tile_tmgp_sg_t_kernel(tc, x, design_points, chol_inv, out):
 
         def pool_terms(i):
             tpool[i] = []
-            for d in ((GIVE_DIM,) + POOL_DIMS if gives(i) else POOL_DIMS):
+            for d in (POOL_DIMS + (LAST_DIM,) if gives(i) else POOL_DIMS):
                 tt = tpoolp.tile([P, M], F32, tag="tpool", name="tpool%d_%d" % (i, d))
                 nc.gpsimd.tensor_scalar(
                     out=tt[:], in0=zc[d], scalar1=BIG, scalar2=xv[:, d, i : i + 1], op0=ALU.min, op1=ALU.max
@@ -241,7 +247,7 @@ def tile_tmgp_sg_t_kernel(tc, x, design_points, chol_inv, out):
                 tpool[i].append(tt)
 
         def transposes(tiles):
-            srcs = {i: [acc[i], tv[i]] + tpool[i][::-1] + tact[i][::-1] for i in tiles}
+            srcs = {i: [acc[i]] + ([] if seeded(i) else [tv[i]]) + tpool[i][::-1] + tact[i][::-1] for i in tiles}
             for i in tiles:
                 lts[i] = ltp.tile([P, M], F32, tag="lt", name="lt%d" % i)
             for t in range(PACK):
@@ -322,13 +328,16 @@ def tile_tmgp_sg_t_kernel(tc, x, design_points, chol_inv, out):
                 quantise(g)
             for d in STEP_DIMS:
                 for i in tiles_of(pr):
-                    if d != GIVE_DIM or not gives(i):
+                    if d != LAST_DIM or not gives(i):
                         dve_step(i, d)
                 if pr == 0 and d == DVE_DIMS[0]:
                     make_rho(0, FIRST)
             for i in tiles_of(pr):
                 act_terms(i)
                 pool_terms(i)
+            for i in tiles_of(pr + 1):
+                if seeded(i):
+                    seed(i)
             if pr == 0:
                 make_rest_of_xv()
             if pr == 1:

@@ -28,7 +28,6 @@ NMAX = 6
 BIG = 3.0e38
 STEP_DIMS = (0, 3, 1, 2)
 LAST_DIM = 3
-KEEP_EVERY = 8
 FIRST = 8
 
 
@@ -202,12 +201,13 @@ def tile_tmgp_sg_t_kernel(tc, x, design_points, chol_inv, out):
         kgs = {}
         qs = {}
         pos = {}
+        obs = {}
 
         def gives(i):
-            return seeded(i) and i // 2 % KEEP_EVERY != KEEP_EVERY - 1
+            return seeded(i)
 
         def seeded(i):
-            return i // 2 % 2 == 1
+            return i % 2 == 1 and i > 1
 
         def seed(i):
             acc[i] = accp.tile([P, M], F32, tag="acc", name="acc%d" % i)
@@ -303,11 +303,12 @@ def tile_tmgp_sg_t_kernel(tc, x, design_points, chol_inv, out):
                     )
                 pos[g].append(po)
 
-        def store(g):
-            ob = obp.tile([P, GROUP, PO], F32, tag="ob", name="ob%d" % g)
-            for h, po in enumerate(pos[g]):
-                nc.scalar.copy(out=ob[:, 2 * h : 2 * h + 2, :], in_=po[:])
-            nc.sync.dma_start(out=out_v[:, g * GROUP : (g + 1) * GROUP, :], in_=ob[:])
+        def copy_out(g, h):
+            if h == 0:
+                obs[g] = obp.tile([P, GROUP, PO], F32, tag="ob", name="ob%d" % g)
+            nc.scalar.copy(out=obs[g][:, 2 * h : 2 * h + 2, :], in_=pos[g][h][:])
+            if h == GROUP // 2 - 1:
+                nc.sync.dma_start(out=out_v[:, g * GROUP : (g + 1) * GROUP, :], in_=obs[g][:])
 
         def tiles_of(pair):
             return [2 * pair, 2 * pair + 1] if 0 <= pair < NPAIR else []
@@ -320,10 +321,6 @@ def tile_tmgp_sg_t_kernel(tc, x, design_points, chol_inv, out):
                 multiply(g)
             if tiles_of(pr - 1):
                 transposes(tiles_of(pr - 1)[::-1])
-            for i in reversed(tiles_of(pr - 2)):
-                expo(i)
-            for g in group_at(pr - 6):
-                store(g)
             for g in group_at(pr - 4):
                 quantise(g)
             for d in STEP_DIMS:
@@ -332,12 +329,20 @@ def tile_tmgp_sg_t_kernel(tc, x, design_points, chol_inv, out):
                         dve_step(i, d)
                 if pr == 0 and d == DVE_DIMS[0]:
                     make_rho(0, FIRST)
-            for i in tiles_of(pr):
+            for i in tiles_of(pr)[0:1]:
+                act_terms(i)
+                pool_terms(i)
+            for i in reversed(tiles_of(pr - 2)):
+                expo(i)
+            for i in tiles_of(pr)[1:2]:
                 act_terms(i)
                 pool_terms(i)
             for i in tiles_of(pr + 1):
                 if seeded(i):
                     seed(i)
+            for h in range(2):
+                for g in group_at(pr - 5 - h):
+                    copy_out(g, h)
             if pr == 0:
                 make_rest_of_xv()
             if pr == 1:

@@ -17,7 +17,6 @@ N, D, M, PO = 16384, 8, 512, 256
 NT = N // P
 PACK = 4
 GROUP = 4
-NG = NT // GROUP
 NPAIR = NT // 2
 FLOPS = 2 * N * M * PO
 
@@ -28,6 +27,9 @@ NMAX = 6
 BIG = 3.0e38
 STEP_DIMS = (0, 3, 1, 2)
 LAST_DIM = 3
+VECTOR_COPIES = 2
+WARM_UP = 14
+LAST_PAIRS = 2
 FIRST = 8
 
 
@@ -44,7 +46,7 @@ def tile_tmgp_sg_t_kernel(tc, x, design_points, chol_inv, out):
         tpoolp = ctx.enter_context(tc.tile_pool(name="tpoolp", bufs=14))
         kgp = ctx.enter_context(tc.tile_pool(name="kgp", bufs=3))
         qp = ctx.enter_context(tc.tile_pool(name="qp", bufs=3))
-        obp = ctx.enter_context(tc.tile_pool(name="obp", bufs=3))
+        obp = ctx.enter_context(tc.tile_pool(name="obp", bufs=6))
         ctx.enter_context(tc.manual_schedule())
 
         z_sb = consts.tile([P, PACK, D], BF16)
@@ -148,6 +150,12 @@ def tile_tmgp_sg_t_kernel(tc, x, design_points, chol_inv, out):
             constant(d)
         rc = zc[D]
 
+        busy = pop.tile([P, M], F32, tag="po", name="busy")
+        for n in range(WARM_UP):
+            nc.tensor.matmul(
+                out=busy[:], lhsT=identb[:], rhs=x_sb[:, 0 : M // D, :].rearrange("p i d -> p (i d)"), start=True, stop=True
+            )
+
         factor = consts.tile([P, D], F32)
         nc.vector.reciprocal(out=factor[:], in_=gb[:, 2 * D : 3 * D])
         shift = consts.tile([P, D], F32)
@@ -203,15 +211,23 @@ def tile_tmgp_sg_t_kernel(tc, x, design_points, chol_inv, out):
         pos = {}
         obs = {}
 
+        def at_end(i):
+            return i // 2 >= NPAIR - LAST_PAIRS
+
         def gives(i):
-            return seeded(i)
+            return seeded(i) and not at_end(i)
 
         def seeded(i):
-            return i % 2 == 1 and i > 1
+            return i % 2 == 1 and i > 1 or at_end(i)
 
         def seed(i):
             acc[i] = accp.tile([P, M], F32, tag="acc", name="acc%d" % i)
-            nc.scalar.activation(out=acc[i][:], in_=rc, func=ACTF.Identity, bias=rho[:, i : i + 1], scale=1.0)
+            if at_end(i) and i % 2 == 1:
+                nc.gpsimd.tensor_scalar(
+                    out=acc[i][:], in0=rc, scalar1=1.0, scalar2=rho[:, i : i + 1], op0=ALU.mult, op1=ALU.add
+                )
+            else:
+                nc.scalar.activation(out=acc[i][:], in_=rc, func=ACTF.Identity, bias=rho[:, i : i + 1], scale=1.0)
 
         def dve_step(i, d):
             if d == LAST_DIM and not seeded(i):
@@ -264,34 +280,43 @@ def tile_tmgp_sg_t_kernel(tc, x, design_points, chol_inv, out):
                                 is_transpose=True,
                             )
 
+        units = [(i, GROUP) for i in range(0, NT - 2 * GROUP, GROUP)]
+        units += [(i, 2) for i in range(NT - 2 * GROUP, NT - 2, 2)] + [(NT - 2, 1), (NT - 1, 1)]
+        unit_of = {i + s: (u, s) for u, (i, size) in enumerate(units) for s in range(size)}
+
         def expo(i):
-            g, s = divmod(i, GROUP)
-            if g not in kgs:
-                kgs[g] = kgp.tile([P, GROUP, P, PACK], BF16, tag="kg", name="kg%d" % g, align_bytes=64)
+            u, s = unit_of[i]
+            if u not in kgs:
+                kgs[u] = kgp.tile([P, units[u][1], P, PACK], BF16, tag="kg", name="kg%d" % u, align_bytes=64)
             nc.scalar.activation(
-                out=kgs[g][:, s, :, :],
+                out=kgs[u][:, s, :, :],
                 in_=lts[i][:].rearrange("p (t n) -> p n t", t=PACK),
                 func=ACTF.Exp,
                 scale=-1.0,
             )
 
-        def quantise(g):
-            codes = qp.tile([P, GROUP * P], U32, tag="codes", name="codes%d" % g, align_bytes=64)
-            scales = qp.tile([P, GROUP * P], U8, tag="scales", name="scales%d" % g, align_bytes=64)
+        def quantise(u):
+            size = units[u][1]
+            codes = qp.tile([P, size * P], U32, tag="codes", name="codes%d" % u, align_bytes=64)
+            scales = qp.tile([P, size * P], U8, tag="scales", name="scales%d" % u, align_bytes=64)
             nc.vector.quantize_mx(
                 out=codes[:].bitcast(FP8X4),
                 scales=scales[:],
-                in_=kgs[g][:].rearrange("p s n t -> p (s n t)"),
+                in_=kgs[u][:].rearrange("p s n t -> p (s n t)"),
             )
-            qs[g] = (codes, scales)
+            qs[u] = (codes, scales)
 
-        def multiply(g):
-            codes, scales = qs[g]
-            pos[g] = []
-            for h in range(GROUP // 2):
-                po = pop.tile([P, 2, PO], F32, tag="po", name="po%d_%d" % (g, h))
-                for e in range(2):
-                    cols = slice((2 * h + e) * P, (2 * h + e + 1) * P)
+        def multiply(u):
+            codes, scales = qs[u]
+            size = units[u][1]
+            pos[u] = []
+            for h in range(0, size, 2):
+                if size > 1:
+                    po = pop.tile([P, 2, PO], F32, tag="po", name="po%d_%d" % (u, h))
+                else:
+                    po = ltp.tile([P, 2, PO], F32, tag="lt", name="po%d_%d" % (u, h))
+                for e in range(min(2, size - h)):
+                    cols = slice((h + e) * P, (h + e + 1) * P)
                     nc.tensor.matmul_mx(
                         out=po[:, e, :],
                         lhsT=codes[:, cols].bitcast(FP8X4),
@@ -301,38 +326,45 @@ def tile_tmgp_sg_t_kernel(tc, x, design_points, chol_inv, out):
                         start=True,
                         stop=True,
                     )
-                pos[g].append(po)
+                pos[u].append(po)
 
-        def copy_out(g, h):
+        def copy_out(u, h):
+            i, size = units[u]
             if h == 0:
-                obs[g] = obp.tile([P, GROUP, PO], F32, tag="ob", name="ob%d" % g)
-            nc.scalar.copy(out=obs[g][:, 2 * h : 2 * h + 2, :], in_=pos[g][h][:])
-            if h == GROUP // 2 - 1:
-                nc.sync.dma_start(out=out_v[:, g * GROUP : (g + 1) * GROUP, :], in_=obs[g][:])
+                obs[u] = obp.tile([P, size, PO], F32, tag="ob", name="ob%d" % u)
+            if size == 1:
+                nc.vector.tensor_copy(out=obs[u][:], in_=pos[u][h][:, 0:1, :])
+            elif h == 1 and u % VECTOR_COPIES == VECTOR_COPIES - 1:
+                nc.vector.tensor_copy(out=obs[u][:, 2 * h : 2 * h + 2, :], in_=pos[u][h][:])
+            else:
+                nc.scalar.copy(out=obs[u][:, 2 * h : 2 * h + 2, :], in_=pos[u][h][:])
+            if 2 * h + 2 >= size:
+                nc.sync.dma_start(out=out_v[:, i : i + size, :], in_=obs[u][:])
 
         def tiles_of(pair):
             return [2 * pair, 2 * pair + 1] if 0 <= pair < NPAIR else []
 
-        def group_at(step):
-            return [step // 2] if step % 2 == 0 and 0 <= step // 2 < NG else []
+        def units_ending(pair):
+            return [u for u, (i, size) in enumerate(units) if i + size - 1 in tiles_of(pair)]
+
+        def steps_of(pair):
+            return [(i, d) for d in STEP_DIMS for i in tiles_of(pair) if d != LAST_DIM or not gives(i)]
 
         for pr in range(NPAIR + 5):
-            for g in group_at(pr - 5):
-                multiply(g)
+            for u in units_ending(pr - 4):
+                multiply(u)
             if tiles_of(pr - 1):
                 transposes(tiles_of(pr - 1)[::-1])
-            for g in group_at(pr - 4):
-                quantise(g)
-            for d in STEP_DIMS:
-                for i in tiles_of(pr):
-                    if d != LAST_DIM or not gives(i):
-                        dve_step(i, d)
-                if pr == 0 and d == DVE_DIMS[0]:
+            for u in units_ending(pr - 3):
+                quantise(u)
+            for n, (i, d) in enumerate(steps_of(pr)):
+                dve_step(i, d)
+                if pr == 0 and n == 1:
                     make_rho(0, FIRST)
             for i in tiles_of(pr)[0:1]:
                 act_terms(i)
                 pool_terms(i)
-            for i in reversed(tiles_of(pr - 2)):
+            for i in tiles_of(pr - 2) if pr - 2 == NPAIR - 1 else tiles_of(pr - 2)[::-1]:
                 expo(i)
             for i in tiles_of(pr)[1:2]:
                 act_terms(i)
@@ -341,8 +373,9 @@ def tile_tmgp_sg_t_kernel(tc, x, design_points, chol_inv, out):
                 if seeded(i):
                     seed(i)
             for h in range(2):
-                for g in group_at(pr - 5 - h):
-                    copy_out(g, h)
+                for u in units_ending(pr - 4 - h):
+                    if 2 * h < units[u][1]:
+                        copy_out(u, h)
             if pr == 0:
                 make_rest_of_xv()
             if pr == 1:

from contextlib import ExitStack

import concourse.mybir as mybir
from concourse.masks import make_identity

F32 = mybir.dt.float32
BF16 = mybir.dt.bfloat16
U32 = mybir.dt.uint32
U8 = mybir.dt.uint8
FP8X4 = mybir.dt.float8_e4m3fn_x4
ALU = mybir.AluOpType
ACTF = mybir.ActivationFunctionType
AX = mybir.AxisListType

P = 128
N, D, M, PO = 16384, 8, 512, 256
NT = N // P
PACK = 4
GROUP = 4
NPAIR = NT // 2
FLOPS = 2 * N * M * PO

DVE_DIMS = (0, 1, 2, 3)
POOL_DIMS = (4, 5)
ACT_DIMS = (6, 7)
NMAX = 6
BIG = 3.0e38
STEP_DIMS = (0, 3, 1, 2)
LAST_DIM = 3
VECTOR_COPIES = 2
WARM_UP = 14
LAST_PAIRS = 2
FIRST = 8


def tile_tmgp_sg_t_kernel(tc, x, design_points, chol_inv, out):
    nc = tc.nc
    with ExitStack() as ctx:
        consts = ctx.enter_context(tc.tile_pool(name="consts", bufs=1))
        zbank = ctx.enter_context(tc.psum_pool(name="zbank", bufs=1))
        ltp = ctx.enter_context(tc.psum_pool(name="ltp", bufs=4))
        pop = ctx.enter_context(tc.psum_pool(name="pop", bufs=2))
        accp = ctx.enter_context(tc.tile_pool(name="accp", bufs=8))
        tvp = ctx.enter_context(tc.tile_pool(name="tvp", bufs=8))
        tactp = ctx.enter_context(tc.tile_pool(name="tactp", bufs=12))
        tpoolp = ctx.enter_context(tc.tile_pool(name="tpoolp", bufs=14))
        kgp = ctx.enter_context(tc.tile_pool(name="kgp", bufs=3))
        qp = ctx.enter_context(tc.tile_pool(name="qp", bufs=3))
        obp = ctx.enter_context(tc.tile_pool(name="obp", bufs=6))
        ctx.enter_context(tc.manual_schedule())

        z_sb = consts.tile([P, PACK, D], BF16)
        nc.scalar.dma_start(out=z_sb[:], in_=design_points.rearrange("(p t) d -> p t d", t=PACK))
        x_sb = consts.tile([P, NT, D], BF16)
        nc.sync.dma_start(out=x_sb[:], in_=x.rearrange("(p i) d -> p i d", p=P))
        c_sb = consts.tile([P, PACK, PO], BF16)
        nc.sync.dma_start(out=c_sb[:], in_=chol_inv.rearrange("(p t) w -> p t w", t=PACK))

        identb = consts.tile([P, P], BF16)
        make_identity(nc, identb[:])
        ident = consts.tile([P, P], F32)
        make_identity(nc, ident[:])

        warm = consts.tile([P, 1], F32)
        nc.vector.memset(warm[:], 0.0)
        nc.scalar.activation(out=warm[:], in_=warm[:], func=ACTF.Exp)

        st = consts.tile([P, P], F32)
        nc.vector.memset(st[:], 0.0)
        sel = consts.tile([P, 3 * D], F32)
        nc.vector.tensor_copy(out=sel[:, 0 : 2 * D], in_=ident[:, 0 : 2 * D])
        nc.vector.tensor_tensor(out=sel[:, 2 * D : 3 * D], in0=ident[:, 0:D], in1=ident[:, D : 2 * D], op=ALU.add)
        nc.vector.tensor_scalar(
            out=sel[:, 2 * D : 2 * D + NMAX], in0=sel[:, 2 * D : 2 * D + NMAX], scalar1=0.5, scalar2=None, op0=ALU.mult
        )
        nc.vector.tensor_scalar(
            out=sel[:, 2 * D + NMAX : 3 * D], in0=sel[:, 2 * D + NMAX : 3 * D], scalar1=-1.0, scalar2=None, op0=ALU.mult
        )

        hi_prev, lo_prev = x_sb, x_sb
        half = NT // 2
        while half >= 16:
            hi_next = consts.tile([P, half, D], BF16, name="hi%d" % half)
            lo_next = consts.tile([P, half, D], BF16, name="lo%d" % half)
            nc.vector.tensor_tensor(
                out=hi_next[:], in0=hi_prev[:, 0:half, :], in1=hi_prev[:, half : 2 * half, :], op=ALU.max
            )
            nc.vector.tensor_tensor(
                out=lo_next[:], in0=lo_prev[:, 0:half, :], in1=lo_prev[:, half : 2 * half, :], op=ALU.min
            )
            hi_prev, lo_prev = hi_next, lo_next
            half //= 2
        low = consts.tile([P, D], F32)
        nc.vector.tensor_reduce(out=low[:], in_=lo_prev[:].rearrange("p i d -> p d i"), axis=AX.X, op=ALU.min)
        nc.vector.tensor_reduce(out=st[:, 0:D], in_=hi_prev[:].rearrange("p i d -> p d i"), axis=AX.X, op=ALU.max)
        nc.vector.tensor_scalar(out=st[:, D : 2 * D], in0=low[:], scalar1=-1.0, scalar2=None, op0=ALU.mult)

        z2b = consts.tile([P, PACK, D], BF16)
        nc.scalar.activation(out=z2b[:], in_=z_sb[:], func=ACTF.Copy, scale=2.0)
        zf = consts.tile([P, PACK, D], F32)
        nc.scalar.activation(out=zf[:], in_=z_sb[:], func=ACTF.Copy)
        z2 = consts.tile([P, PACK, D], F32)
        nc.scalar.activation(out=z2[:], in_=z_sb[:], func=ACTF.Copy, scale=2.0)
        zsum = consts.tile([P, PACK], F32)
        nc.vector.tensor_reduce(out=zsum[:], in_=zf[:, :, 0:NMAX], axis=AX.X, op=ALU.add)
        rz = consts.tile([P, PACK], F32)
        nc.vector.tensor_scalar(out=rz[:], in0=zsum[:], scalar1=-1.0, scalar2=None, op0=ALU.mult)

        def spread(bank, column_of, identity):
            for t in range(PACK):
                nc.tensor.transpose(
                    out=bank[:, t * P : (t + 1) * P],
                    in_=column_of(t).to_broadcast([P, P]),
                    identity=identity[:],
                )

        zp = {}
        for h in range(len(DVE_DIMS) // 2):
            zres = zbank.tile([P, 2, M], BF16, name="zres%d" % h)
            for e in range(2):
                d = DVE_DIMS[2 * h + e]
                spread(zres[:, e, :], lambda t, d=d: z2b[:, t, d : d + 1], identb)
                zp[d] = zres[:, e, :]

        zc = {}

        def constant(d):
            tmp = ltp.tile([P, M], F32, tag="lt", name="ztmp%d" % d)
            if d == D:
                spread(tmp, lambda t: rz[:, t : t + 1], ident)
            elif d < NMAX:
                spread(tmp, lambda t: z2[:, t, d : d + 1], ident)
            else:
                spread(tmp, lambda t: zf[:, t, d : d + 1], ident)
            zs = consts.tile([P, M], F32, name="zs%d" % d)
            nc.scalar.copy(out=zs[:], in_=tmp[:])
            zc[d] = zs[:]

        constant(ACT_DIMS[0])
        stT = pop.tile([P, M], F32, tag="po", name="stT")
        nc.tensor.transpose(out=stT[:, 0:P], in_=st[:], identity=ident[:])
        gcol = consts.tile([P, 1], F32)
        nc.vector.tensor_reduce(out=gcol[:], in_=stT[:, 0:P], axis=AX.X, op=ALU.max)
        constant(ACT_DIMS[1])
        gb = pop.tile([P, M], F32, tag="po", name="gb")
        nc.tensor.matmul(
            out=gb[:, 0 : 3 * D], lhsT=gcol[:, 0:1].to_broadcast([P, P]), rhs=sel[:], start=True, stop=True
        )
        for d in (D,) + POOL_DIMS + (LAST_DIM,):
            constant(d)
        rc = zc[D]

        busy = pop.tile([P, M], F32, tag="po", name="busy")
        for n in range(WARM_UP):
            nc.tensor.matmul(
                out=busy[:], lhsT=identb[:], rhs=x_sb[:, 0 : M // D, :].rearrange("p i d -> p (i d)"), start=True, stop=True
            )

        factor = consts.tile([P, D], F32)
        nc.vector.reciprocal(out=factor[:], in_=gb[:, 2 * D : 3 * D])
        shift = consts.tile([P, D], F32)
        nc.vector.tensor_tensor(out=shift[:], in0=gb[:, D : 2 * D], in1=factor[:], op=ALU.mult)
        xv = consts.tile([P, D, NT], F32)
        first = xv[:, :, 0:FIRST]
        nc.vector.tensor_tensor(
            out=first, in0=x_sb[:, 0:FIRST, :].rearrange("p i d -> p d i"),
            in1=factor[:].unsqueeze(2).to_broadcast([P, D, FIRST]), op=ALU.mult,
        )
        nc.vector.tensor_tensor(
            out=first, in0=first, in1=shift[:].unsqueeze(2).to_broadcast([P, D, FIRST]), op=ALU.add
        )
        rho = consts.tile([P, NT], F32)
        xsum = consts.tile([P, NT], F32)

        def make_rest_of_xv():
            for d in range(D):
                nc.scalar.activation(
                    out=xv[:, d, FIRST:NT], in_=x_sb[:, FIRST:NT, d], func=ACTF.Identity,
                    scale=factor[:, d : d + 1], bias=shift[:, d : d + 1],
                )

        def make_rho(lo, hi):
            nc.vector.tensor_reduce(
                out=xsum[:, lo:hi], in_=xv[:, 0:NMAX, lo:hi].rearrange("p d i -> p i d"), axis=AX.X, op=ALU.add
            )
            nc.vector.tensor_scalar(out=rho[:, lo:hi], in0=xsum[:, lo:hi], scalar1=-0.5, scalar2=None, op0=ALU.mult)

        cg = consts.tile([P, PO, PACK], BF16, align_bytes=64)
        c_codes = consts.tile([P, PO], U32, align_bytes=64)
        c_scales = consts.tile([P, PO], U8, align_bytes=64)

        def interleave_c():
            nc.scalar.copy(out=cg[:], in_=c_sb[:].rearrange("p t w -> p w t"))

        def quantise_c():
            nc.vector.quantize_mx(
                out=c_codes[:].bitcast(FP8X4),
                scales=c_scales[:],
                in_=cg[:].rearrange("p w t -> p (w t)"),
            )

        out_v = out.rearrange("(p i) w -> p i w", p=P)

        acc = {}
        tv = {}
        tact = {}
        tpool = {}
        lts = {}
        kgs = {}
        qs = {}
        pos = {}
        obs = {}

        def at_end(i):
            return i // 2 >= NPAIR - LAST_PAIRS

        def gives(i):
            return seeded(i) and not at_end(i)

        def seeded(i):
            return i % 2 == 1 and i > 1 or at_end(i)

        def seed(i):
            acc[i] = accp.tile([P, M], F32, tag="acc", name="acc%d" % i)
            if at_end(i) and i % 2 == 1:
                nc.gpsimd.tensor_scalar(
                    out=acc[i][:], in0=rc, scalar1=1.0, scalar2=rho[:, i : i + 1], op0=ALU.mult, op1=ALU.add
                )
            else:
                nc.scalar.activation(out=acc[i][:], in_=rc, func=ACTF.Identity, bias=rho[:, i : i + 1], scale=1.0)

        def dve_step(i, d):
            if d == LAST_DIM and not seeded(i):
                tv[i] = tvp.tile([P, M], F32, tag="tv", name="tv%d" % i)
                nc.vector.tensor_scalar(
                    out=tv[i][:], in0=zp[d], scalar1=xv[:, d, i : i + 1], scalar2=rho[:, i : i + 1],
                    op0=ALU.max, op1=ALU.add,
                )
                return
            if d == DVE_DIMS[0] and not seeded(i):
                acc[i] = accp.tile([P, M], F32, tag="acc", name="acc%d" % i)
                prior = rc
            else:
                prior = acc[i][:]
            nc.vector.scalar_tensor_tensor(
                out=acc[i][:], in0=zp[d], scalar=xv[:, d, i : i + 1], in1=prior, op0=ALU.max, op1=ALU.add
            )

        def act_terms(i):
            tact[i] = []
            for d in ACT_DIMS:
                tt = tactp.tile([P, M], F32, tag="tact", name="tact%d_%d" % (i, d))
                nc.scalar.activation(out=tt[:], in_=zc[d], func=ACTF.Abs, bias=xv[:, d, i : i + 1], scale=1.0)
                tact[i].append(tt)

        def pool_terms(i):
            tpool[i] = []
            for d in (POOL_DIMS + (LAST_DIM,) if gives(i) else POOL_DIMS):
                tt = tpoolp.tile([P, M], F32, tag="tpool", name="tpool%d_%d" % (i, d))
                nc.gpsimd.tensor_scalar(
                    out=tt[:], in0=zc[d], scalar1=BIG, scalar2=xv[:, d, i : i + 1], op0=ALU.min, op1=ALU.max
                )
                tpool[i].append(tt)

        def transposes(tiles):
            srcs = {i: [acc[i]] + ([] if seeded(i) else [tv[i]]) + tpool[i][::-1] + tact[i][::-1] for i in tiles}
            for i in tiles:
                lts[i] = ltp.tile([P, M], F32, tag="lt", name="lt%d" % i)
            for t in range(PACK):
                cols = slice(t * P, (t + 1) * P)
                for j in range(max(len(srcs[i]) for i in tiles)):
                    for i in tiles:
                        if j < len(srcs[i]):
                            nc.tensor.matmul(
                                out=lts[i][:, cols],
                                lhsT=srcs[i][j][:, cols],
                                rhs=ident[:],
                                start=(j == 0),
                                stop=(j == len(srcs[i]) - 1),
                                is_transpose=True,
                            )

        units = [(i, GROUP) for i in range(0, NT - 2 * GROUP, GROUP)]
        units += [(i, 2) for i in range(NT - 2 * GROUP, NT - 2, 2)] + [(NT - 2, 1), (NT - 1, 1)]
        unit_of = {i + s: (u, s) for u, (i, size) in enumerate(units) for s in range(size)}

        def expo(i):
            u, s = unit_of[i]
            if u not in kgs:
                kgs[u] = kgp.tile([P, units[u][1], P, PACK], BF16, tag="kg", name="kg%d" % u, align_bytes=64)
            nc.scalar.activation(
                out=kgs[u][:, s, :, :],
                in_=lts[i][:].rearrange("p (t n) -> p n t", t=PACK),
                func=ACTF.Exp,
                scale=-1.0,
            )

        def quantise(u):
            size = units[u][1]
            codes = qp.tile([P, size * P], U32, tag="codes", name="codes%d" % u, align_bytes=64)
            scales = qp.tile([P, size * P], U8, tag="scales", name="scales%d" % u, align_bytes=64)
            nc.vector.quantize_mx(
                out=codes[:].bitcast(FP8X4),
                scales=scales[:],
                in_=kgs[u][:].rearrange("p s n t -> p (s n t)"),
            )
            qs[u] = (codes, scales)

        def multiply(u):
            codes, scales = qs[u]
            size = units[u][1]
            pos[u] = []
            for h in range(0, size, 2):
                if size > 1:
                    po = pop.tile([P, 2, PO], F32, tag="po", name="po%d_%d" % (u, h))
                else:
                    po = ltp.tile([P, 2, PO], F32, tag="lt", name="po%d_%d" % (u, h))
                for e in range(min(2, size - h)):
                    cols = slice((h + e) * P, (h + e + 1) * P)
                    nc.tensor.matmul_mx(
                        out=po[:, e, :],
                        lhsT=codes[:, cols].bitcast(FP8X4),
                        lhsT_scale=scales[:, cols],
                        rhs=c_codes[:].bitcast(FP8X4),
                        rhs_scale=c_scales[:],
                        start=True,
                        stop=True,
                    )
                pos[u].append(po)

        def copy_out(u, h):
            i, size = units[u]
            if h == 0:
                obs[u] = obp.tile([P, size, PO], F32, tag="ob", name="ob%d" % u)
            if size == 1:
                nc.vector.tensor_copy(out=obs[u][:], in_=pos[u][h][:, 0:1, :])
            elif h == 1 and u % VECTOR_COPIES == VECTOR_COPIES - 1:
                nc.vector.tensor_copy(out=obs[u][:, 2 * h : 2 * h + 2, :], in_=pos[u][h][:])
            else:
                nc.scalar.copy(out=obs[u][:, 2 * h : 2 * h + 2, :], in_=pos[u][h][:])
            if 2 * h + 2 >= size:
                nc.sync.dma_start(out=out_v[:, i : i + size, :], in_=obs[u][:])

        def tiles_of(pair):
            return [2 * pair, 2 * pair + 1] if 0 <= pair < NPAIR else []

        def units_ending(pair):
            return [u for u, (i, size) in enumerate(units) if i + size - 1 in tiles_of(pair)]

        def steps_of(pair):
            return [(i, d) for d in STEP_DIMS for i in tiles_of(pair) if d != LAST_DIM or not gives(i)]

        for pr in range(NPAIR + 5):
            for u in units_ending(pr - 4):
                multiply(u)
            if tiles_of(pr - 1):
                transposes(tiles_of(pr - 1)[::-1])
            for u in units_ending(pr - 3):
                quantise(u)
            for n, (i, d) in enumerate(steps_of(pr)):
                dve_step(i, d)
                if pr == 0 and n == 1:
                    make_rho(0, FIRST)
            for i in tiles_of(pr)[0:1]:
                act_terms(i)
                pool_terms(i)
            for i in tiles_of(pr - 2) if pr - 2 == NPAIR - 1 else tiles_of(pr - 2)[::-1]:
                expo(i)
            for i in tiles_of(pr)[1:2]:
                act_terms(i)
                pool_terms(i)
            for i in tiles_of(pr + 1):
                if seeded(i):
                    seed(i)
            for h in range(2):
                for u in units_ending(pr - 4 - h):
                    if 2 * h < units[u][1]:
                        copy_out(u, h)
            if pr == 0:
                make_rest_of_xv()
            if pr == 1:
                make_rho(FIRST, NT)
                interleave_c()
            if pr == 2:
                quantise_c()
